import numpy as np
import ml_dtypes


def mxq(x, axis, fmt="e4m3"):
    dtype, down = {"e4m3": (ml_dtypes.float8_e4m3fn, 7), "e5m2": (ml_dtypes.float8_e5m2, 14)}[fmt]
    v = np.moveaxis(np.asarray(x, np.float32).astype(ml_dtypes.bfloat16).astype(np.float64), axis, -1)
    blocks = v.reshape(v.shape[:-1] + (-1, 32))
    amax = np.abs(blocks).max(-1, keepdims=True)
    byte = np.maximum(np.where(amax > 0, np.frexp(amax)[1] - 1 + 127, 0) - down, 1)
    scale = np.exp2(byte - 127.0)
    codes = (blocks / scale).astype(np.float32).astype(dtype).astype(np.float64)
    return np.moveaxis((codes * scale).reshape(v.shape), -1, axis)


WIDE = False


def mx_kscale(k):
    if not WIDE:
        return np.ones(k)
    levels = np.array([10, -10, 5, -5, 0])
    a = np.random.permutation(np.resize(levels, k // 512 * 4)).reshape(k // 512, 4)
    idx = np.arange(k)
    return np.exp2(a[idx // 512, idx % 128 // 32])


BF16 = ml_dtypes.bfloat16


def bf(x):
    return np.asarray(x, np.float32).astype(BF16)


def f64(x):
    return np.asarray(x).astype(np.float64)


N, C, T, V, H, O = 2, 1024, 64, 25, 512, 1024


def setup_inputs():
    s = mx_kscale(C)
    wscale = 0.7 * np.sqrt(V / C)
    return {
        "xm": bf(np.random.standard_normal((N, C, T)) / np.sqrt(V) * s[None, :, None]),
        "Wq": bf(np.random.standard_normal((H, C)) * wscale / s[None, :]),
        "bq": bf(np.random.standard_normal(H) * 0.3),
        "Wk": bf(np.random.standard_normal((H, C)) * wscale / s[None, :]),
        "bk": bf(np.random.standard_normal(H) * 0.3),
        "Wr": bf(np.random.standard_normal((O, H)) / np.sqrt(H)),
        "br": bf(np.random.standard_normal(O) * 0.3),
    }


def reference(xm, Wq, bq, Wk, bk, Wr, br):
    xq = mxq(f64(xm), 1, "e4m3")
    q = (mxq(f64(Wq), 1, "e4m3") @ xq) + f64(bq)[None, :, None]
    k = (mxq(f64(Wk), 1, "e4m3") @ xq) + f64(bk)[None, :, None]
    d = np.tanh(q[:, :, :, None] - k[:, :, None, :])
    m = mxq(f64(Wr), 1, "e4m3") @ mxq(d, 1, "e4m3").reshape(N, H, T * T)
    return m.reshape(N, O, T, T) + f64(br)[None, :, None, None]

@@ -1,0 +1,259 @@
+from contextlib import ExitStack
+
+import concourse.mybir as mybir
+from concourse.masks import make_identity
+
+F32 = mybir.dt.float32
+BF16 = mybir.dt.bfloat16
+U32 = mybir.dt.uint32
+U8 = mybir.dt.uint8
+FP8X4 = mybir.dt.float8_e4m3fn_x4
+ALU = mybir.AluOpType
+ACT = mybir.ActivationFunctionType
+
+SAMPLES, C, T, H, O = 2, 1024, 64, 512, 1024
+
+P = 128
+PACK = 4
+K_PASS = P * PACK
+C_PASSES = C // K_PASS
+H_TILES = H // P
+O_TILES = O // P
+BANK = 512
+PAIRS = 2
+
+FRAMES = BANK // T
+CHUNKS_PER_SAMPLE = T // FRAMES
+CHUNKS = SAMPLES * CHUNKS_PER_SAMPLE
+
+GROUP = 2
+LEAD = GROUP + 1
+VECTOR_FRAMES = 2
+
+FLOPS = 2 * 2 * SAMPLES * H * C * T + 2 * SAMPLES * O * H * T * T
+
+
+def tile_ta_block_pa_kernel(tc, xm, Wq, bq, Wk, bk, Wr, br, out):
+    nc = tc.nc
+    with ExitStack() as ctx:
+        keep = ctx.enter_context(tc.tile_pool(name="keep", bufs=1))
+        diffs = ctx.enter_context(tc.tile_pool(name="diffs", bufs=3))
+        tanhs = ctx.enter_context(tc.tile_pool(name="tanhs", bufs=3))
+        quantised = ctx.enter_context(tc.tile_pool(name="quantised", bufs=2 * GROUP + 2))
+        stages = ctx.enter_context(tc.tile_pool(name="stages", bufs=6))
+        banks = ctx.enter_context(tc.psum_pool(name="banks", bufs=8))
+
+        x_raw = keep.tile([P, SAMPLES * C_PASSES * PACK * T], BF16, name="x_raw")
+        x_raw_v = x_raw[:].rearrange("p (n b et) -> p n b et", n=SAMPLES, b=C_PASSES * PAIRS)
+        for n in range(SAMPLES):
+            nc.sync.dma_start(
+                out=x_raw_v[:, n], in_=xm[n].rearrange("(b p e) t -> p b (e t)", p=P, e=2)
+            )
+
+        proj_raw = {}
+        for name, w in (("q", Wq), ("k", Wk)):
+            proj_raw[name] = keep.tile([P, H_TILES * C], BF16, name="raw_" + name)
+            for u in range(PAIRS):
+                nc.sync.dma_start(
+                    out=proj_raw[name][:, 2 * u * C : 2 * (u + 1) * C],
+                    in_=w[2 * P * u : 2 * P * (u + 1), :].rearrange("(p e) c -> p (e c)", e=2),
+                )
+
+        wr_raw = keep.tile([P, O_TILES * H], BF16, name="wr_raw")
+        nc.sync.dma_start(out=wr_raw[:], in_=Wr.rearrange("(p a) h -> p (a h)", a=O_TILES))
+
+        bias_bf = {}
+        for name, b in (("q", bq), ("k", bk)):
+            bias_bf[name] = keep.tile([P, PACK], BF16, name="bias_" + name)
+            nc.scalar.dma_start(
+                out=bias_bf[name][:].rearrange("p (u e) -> p u e", e=2),
+                in_=b.rearrange("(u p e) -> p u e", p=P, e=2),
+            )
+        br_bf = keep.tile([P, O_TILES], BF16, name="br_bf")
+        nc.scalar.dma_start(out=br_bf[:], in_=br.rearrange("(p a) -> p a", a=O_TILES))
+
+        ident = keep.tile([P, P], F32, name="ident")
+        make_identity(nc, ident[:])
+
+        warm = keep.tile([P, 2], F32, name="warm")
+        nc.vector.memset(warm[:], 0.0)
+        nc.scalar.activation(out=warm[:, 1:2], in_=warm[:, 0:1], func=ACT.Tanh)
+
+        br_f32 = keep.tile([P, O_TILES], F32, name="br_f32")
+        nc.vector.tensor_copy(out=br_f32[:], in_=br_bf[:])
+
+        x_grouped = keep.tile([P, C_PASSES * SAMPLES * T * PACK], BF16, name="x_grouped", align_bytes=64)
+        x_grouped_v = x_grouped[:].rearrange(
+            "p (g n t j) -> p g n t j", g=C_PASSES, n=SAMPLES, j=PACK
+        )
+        x_values = x_raw[:].rearrange("p (n g j t) -> p n g j t", n=SAMPLES, g=C_PASSES, j=PACK)
+        for n in range(SAMPLES):
+            nc.vector.tensor_copy(
+                out=x_grouped_v[:, :, n], in_=x_values[:, n].rearrange("p g j t -> p g t j")
+            )
+        x_cols = SAMPLES * T
+        x_words = keep.tile([P, C_PASSES * x_cols], U32, name="x_words", align_bytes=64)
+        x_scales = keep.tile([P, C_PASSES * x_cols], U8, name="x_scales", align_bytes=64)
+        nc.vector.quantize_mx(out=x_words[:].bitcast(FP8X4), scales=x_scales[:], in_=x_grouped[:])
+
+        def turn_rows(raw_words, first_word, planes, grouped_words, copy):
+            bank = banks.tile([P, BANK], F32, name="bank")
+            for b in range(planes):
+                nc.tensor.transpose(
+                    bank[:, b * P : (b + 1) * P],
+                    raw_words[:, first_word + b * P : first_word + (b + 1) * P],
+                    ident[:],
+                )
+            copy(
+                out=grouped_words.rearrange("p (x m u) -> p x m u", m=P, u=PAIRS),
+                in_=bank[:].rearrange("p (x u m) -> p x m u", m=P, u=PAIRS),
+            )
+
+        copies = (nc.scalar.copy, nc.vector.tensor_copy)
+
+        tile_cols = C_PASSES * P
+        proj_words = {}
+        proj_scales = {}
+        for name in ("q", "k"):
+            raw_words = proj_raw[name][:].bitcast(F32)
+            grouped = keep.tile([P, H_TILES * tile_cols * PACK], BF16, name="grouped_" + name, align_bytes=64)
+            grouped_words = grouped[:].bitcast(F32)
+            proj_words[name] = keep.tile([P, H_TILES * tile_cols], U32, name="words_" + name, align_bytes=64)
+            proj_scales[name] = keep.tile([P, H_TILES * tile_cols], U8, name="scales_" + name, align_bytes=64)
+            for u in range(PAIRS):
+                for j in (2 * u, 2 * u + 1):
+                    turn_rows(
+                        raw_words,
+                        j * (C // 2),
+                        C_PASSES * PAIRS,
+                        grouped_words[:, j * tile_cols * PAIRS : (j + 1) * tile_cols * PAIRS],
+                        copies[j % 2],
+                    )
+                cols = slice(2 * u * tile_cols, 2 * (u + 1) * tile_cols)
+                nc.vector.quantize_mx(
+                    out=proj_words[name][:, cols].bitcast(FP8X4),
+                    scales=proj_scales[name][:, cols],
+                    in_=grouped[:, 2 * u * tile_cols * PACK : 2 * (u + 1) * tile_cols * PACK],
+                )
+
+        proj = {}
+        for name in ("q", "k"):
+            bank = banks.tile([P, BANK], F32, name="bank")
+            for j in range(H_TILES):
+                for g in range(C_PASSES):
+                    w_cols = slice((j * C_PASSES + g) * P, (j * C_PASSES + g + 1) * P)
+                    nc.tensor.matmul_mx(
+                        out=bank[:, j * x_cols : (j + 1) * x_cols],
+                        lhsT=proj_words[name][:, w_cols].bitcast(FP8X4),
+                        lhsT_scale=proj_scales[name][:, w_cols],
+                        rhs=x_words[:, g * x_cols : (g + 1) * x_cols].bitcast(FP8X4),
+                        rhs_scale=x_scales[:, g * x_cols : (g + 1) * x_cols],
+                        start=(g == 0),
+                        stop=(g == C_PASSES - 1),
+                    )
+            proj[name] = keep.tile([P, x_cols * PACK], F32, name="proj_" + name)
+            nc.vector.tensor_tensor(
+                out=proj[name][:].rearrange("p (c j) -> p c j", j=PACK),
+                in0=bank[:].rearrange("p (j c) -> p c j", j=PACK),
+                in1=bias_bf[name][:].unsqueeze(1).to_broadcast([P, x_cols, PACK]),
+                op=ALU.add,
+            )
+        q_v = proj["q"][:].rearrange("p (n g j) -> p n g j", n=SAMPLES, j=PACK)
+        k_v = proj["k"][:].rearrange("p (n t j) -> p n t j", n=SAMPLES, j=PACK)
+
+        diff_of = {}
+        d_words_of = {}
+        d_scales_of = {}
+
+        def subtract(chunk):
+            n, part = divmod(chunk, CHUNKS_PER_SAMPLE)
+            diff_of[chunk] = diffs.tile([P, BANK * PACK], F32, name="diff")
+            diff_v = diff_of[chunk][:].rearrange("p (g t j) -> p g t j", t=T, j=PACK)
+            for engine, lo, hi in (
+                (nc.vector, 0, VECTOR_FRAMES),
+                (nc.gpsimd, VECTOR_FRAMES, FRAMES),
+            ):
+                shape = [P, hi - lo, T, PACK]
+                first = part * FRAMES
+                engine.tensor_tensor(
+                    out=diff_v[:, lo:hi],
+                    in0=q_v[:, n, first + lo : first + hi, :].unsqueeze(2).to_broadcast(shape),
+                    in1=k_v[:, n].unsqueeze(1).to_broadcast(shape),
+                    op=ALU.subtract,
+                )
+
+        def tanh_and_quantise(chunk):
+            d_bf = tanhs.tile([P, BANK * PACK], BF16, name="d_bf", align_bytes=64)
+            nc.scalar.activation(out=d_bf[:], in_=diff_of[chunk][:], func=ACT.Tanh)
+            d_words_of[chunk] = quantised.tile([P, BANK], U32, name="d_words", align_bytes=64)
+            d_scales_of[chunk] = quantised.tile([P, BANK], U8, name="d_scales", align_bytes=64)
+            nc.vector.quantize_mx(
+                out=d_words_of[chunk][:].bitcast(FP8X4), scales=d_scales_of[chunk][:], in_=d_bf[:]
+            )
+
+        def make_chunk(chunk):
+            if chunk + 1 < CHUNKS:
+                subtract(chunk + 1)
+            if chunk < CHUNKS:
+                tanh_and_quantise(chunk)
+
+        subtract(0)
+
+        wr_words_raw = wr_raw[:].bitcast(F32)
+        wr_grouped = keep.tile([P, O * PACK], BF16, name="wr_grouped", align_bytes=64)
+        wr_grouped_words = wr_grouped[:].bitcast(F32)
+        for pair in range(O_TILES // 2):
+            turn_rows(
+                wr_words_raw,
+                pair * H,
+                2 * PAIRS,
+                wr_grouped_words[:, pair * 2 * P * PAIRS : (pair + 1) * 2 * P * PAIRS],
+                copies[pair % 2],
+            )
+        wr_words = keep.tile([P, O], U32, name="wr_words", align_bytes=64)
+        wr_scales = keep.tile([P, O], U8, name="wr_scales", align_bytes=64)
+        nc.vector.quantize_mx(out=wr_words[:].bitcast(FP8X4), scales=wr_scales[:], in_=wr_grouped[:])
+
+        for chunk in range(LEAD):
+            make_chunk(chunk)
+
+        out_v = out.rearrange("n (p a) g t -> n p a (g t)", a=O_TILES)
+        banks_done = 0
+        for group in range(CHUNKS // GROUP):
+            n, part = divmod(group * GROUP, CHUNKS_PER_SAMPLE)
+            for a in range(O_TILES):
+                stage = stages.tile([P, GROUP * BANK], F32, name="stage")
+                for i in range(GROUP):
+                    chunk = group * GROUP + i
+                    bank = banks.tile([P, BANK], F32, name="bank")
+                    nc.tensor.matmul_mx(
+                        out=bank[:],
+                        lhsT=wr_words[:, a * P : (a + 1) * P].bitcast(FP8X4),
+                        lhsT_scale=wr_scales[:, a * P : (a + 1) * P],
+                        rhs=d_words_of[chunk][:].bitcast(FP8X4),
+                        rhs_scale=d_scales_of[chunk][:],
+                        start=True,
+                        stop=True,
+                    )
+                    if (banks_done % 8) % 3 == 0:
+                        nc.scalar.activation(
+                            out=stage[:, i * BANK : (i + 1) * BANK],
+                            in_=bank[:],
+                            func=ACT.Identity,
+                            bias=br_f32[:, a : a + 1],
+                            scale=1.0,
+                        )
+                    else:
+                        nc.vector.tensor_scalar(
+                            out=stage[:, i * BANK : (i + 1) * BANK],
+                            in0=bank[:],
+                            scalar1=br_f32[:, a : a + 1],
+                            scalar2=None,
+                            op0=ALU.add,
+                        )
+                    banks_done += 1
+                nc.sync.dma_start(
+                    out=out_v[n, :, a, part * BANK : (part + GROUP) * BANK], in_=stage[:]
+                )
+                if banks_done % 8 == 0:
+                    make_chunk(LEAD + banks_done // 8 - 1)

@@ -15,20 +15,23 @@ SAMPLES, C, T, H, O = 2, 1024, 64, 512, 1024
 
 P = 128
 PACK = 4
+PAIRS = 2
 K_PASS = P * PACK
 C_PASSES = C // K_PASS
 H_TILES = H // P
 O_TILES = O // P
 BANK = 512
-PAIRS = 2
 
-FRAMES = BANK // T
-CHUNKS_PER_SAMPLE = T // FRAMES
-CHUNKS = SAMPLES * CHUNKS_PER_SAMPLE
+BANKS_PER_BLOCK = 2
+BLOCK = BANKS_PER_BLOCK * BANK
+FRAMES = BLOCK // T
+BLOCKS_PER_SAMPLE = T // FRAMES
+BLOCKS = SAMPLES * BLOCKS_PER_SAMPLE
+FRAME = T * PACK
 
-GROUP = 2
-LEAD = GROUP + 1
-VECTOR_FRAMES = 2
+VECTOR_FRAMES = 6
+TANH_AT = (1, 4)
+QUANTISE_AT = 6
 
 FLOPS = 2 * 2 * SAMPLES * H * C * T + 2 * SAMPLES * O * H * T * T
 
@@ -36,12 +39,13 @@ FLOPS = 2 * 2 * SAMPLES * H * C * T + 2 * SAMPLES * O * H * T * T
 def tile_ta_block_pa_kernel(tc, xm, Wq, bq, Wk, bk, Wr, br, out):
     nc = tc.nc
     with ExitStack() as ctx:
+        ctx.enter_context(tc.manual_schedule())
         keep = ctx.enter_context(tc.tile_pool(name="keep", bufs=1))
-        diffs = ctx.enter_context(tc.tile_pool(name="diffs", bufs=3))
-        tanhs = ctx.enter_context(tc.tile_pool(name="tanhs", bufs=3))
-        quantised = ctx.enter_context(tc.tile_pool(name="quantised", bufs=2 * GROUP + 2))
-        stages = ctx.enter_context(tc.tile_pool(name="stages", bufs=6))
-        banks = ctx.enter_context(tc.psum_pool(name="banks", bufs=8))
+        works = ctx.enter_context(tc.tile_pool(name="works", bufs=2))
+        quantised = ctx.enter_context(tc.tile_pool(name="quantised", bufs=3))
+        stages = ctx.enter_context(tc.tile_pool(name="stages", bufs=8))
+        k_banks = ctx.enter_context(tc.psum_pool(name="k_banks", bufs=1))
+        banks = ctx.enter_context(tc.psum_pool(name="banks", bufs=7))
 
         x_raw = keep.tile([P, SAMPLES * C_PASSES * PACK * T], BF16, name="x_raw")
         x_raw_v = x_raw[:].rearrange("p (n b et) -> p n b et", n=SAMPLES, b=C_PASSES * PAIRS)
@@ -79,9 +83,6 @@ def tile_ta_block_pa_kernel(tc, xm, Wq, bq, Wk, bk, Wr, br, out):
         nc.vector.memset(warm[:], 0.0)
         nc.scalar.activation(out=warm[:, 1:2], in_=warm[:, 0:1], func=ACT.Tanh)
 
-        br_f32 = keep.tile([P, O_TILES], F32, name="br_f32")
-        nc.vector.tensor_copy(out=br_f32[:], in_=br_bf[:])
-
         x_grouped = keep.tile([P, C_PASSES * SAMPLES * T * PACK], BF16, name="x_grouped", align_bytes=64)
         x_grouped_v = x_grouped[:].rearrange(
             "p (g n t j) -> p g n t j", g=C_PASSES, n=SAMPLES, j=PACK
@@ -96,9 +97,16 @@ def tile_ta_block_pa_kernel(tc, xm, Wq, bq, Wk, bk, Wr, br, out):
         x_scales = keep.tile([P, C_PASSES * x_cols], U8, name="x_scales", align_bytes=64)
         nc.vector.quantize_mx(out=x_words[:].bitcast(FP8X4), scales=x_scales[:], in_=x_grouped[:])
 
-        def turn_rows(raw_words, first_word, planes, grouped_words, copy):
+        bias_qk = keep.tile([P, PACK], F32, name="bias_qk")
+        nc.vector.tensor_tensor(
+            out=bias_qk[:], in0=bias_bf["q"][:], in1=bias_bf["k"][:], op=ALU.subtract
+        )
+        br_f32 = keep.tile([P, O_TILES], F32, name="br_f32")
+        nc.vector.tensor_copy(out=br_f32[:], in_=br_bf[:])
+
+        def turn_rows(raw_words, first_word, grouped_words, copy):
             bank = banks.tile([P, BANK], F32, name="bank")
-            for b in range(planes):
+            for b in range(BANK // P):
                 nc.tensor.transpose(
                     bank[:, b * P : (b + 1) * P],
                     raw_words[:, first_word + b * P : first_word + (b + 1) * P],
@@ -125,7 +133,6 @@ def tile_ta_block_pa_kernel(tc, xm, Wq, bq, Wk, bk, Wr, br, out):
                     turn_rows(
                         raw_words,
                         j * (C // 2),
-                        C_PASSES * PAIRS,
                         grouped_words[:, j * tile_cols * PAIRS : (j + 1) * tile_cols * PAIRS],
                         copies[j % 2],
                     )
@@ -136,9 +143,7 @@ def tile_ta_block_pa_kernel(tc, xm, Wq, bq, Wk, bk, Wr, br, out):
                     in_=grouped[:, 2 * u * tile_cols * PACK : 2 * (u + 1) * tile_cols * PACK],
                 )
 
-        proj = {}
-        for name in ("q", "k"):
-            bank = banks.tile([P, BANK], F32, name="bank")
+        def project(name, bank):
             for j in range(H_TILES):
                 for g in range(C_PASSES):
                     w_cols = slice((j * C_PASSES + g) * P, (j * C_PASSES + g + 1) * P)
@@ -151,53 +156,76 @@ def tile_ta_block_pa_kernel(tc, xm, Wq, bq, Wk, bk, Wr, br, out):
                         start=(g == 0),
                         stop=(g == C_PASSES - 1),
                     )
-            proj[name] = keep.tile([P, x_cols * PACK], F32, name="proj_" + name)
-            nc.vector.tensor_tensor(
-                out=proj[name][:].rearrange("p (c j) -> p c j", j=PACK),
-                in0=bank[:].rearrange("p (j c) -> p c j", j=PACK),
-                in1=bias_bf[name][:].unsqueeze(1).to_broadcast([P, x_cols, PACK]),
-                op=ALU.add,
-            )
-        q_v = proj["q"][:].rearrange("p (n g j) -> p n g j", n=SAMPLES, j=PACK)
-        k_v = proj["k"][:].rearrange("p (n t j) -> p n t j", n=SAMPLES, j=PACK)
+
+        q_bank = banks.tile([P, BANK], F32, name="bank")
+        project("q", q_bank)
+        k_bank = k_banks.tile([P, BANK], F32, name="k_bank")
+        project("k", k_bank)
+        q_sb = keep.tile([P, x_cols * PACK], F32, name="q_sb")
+        nc.vector.tensor_tensor(
+            out=q_sb[:].rearrange("p (c j) -> p c j", j=PACK),
+            in0=q_bank[:].rearrange("p (j c) -> p c j", j=PACK),
+            in1=bias_qk[:].unsqueeze(1).to_broadcast([P, x_cols, PACK]),
+            op=ALU.add,
+        )
+        k_sb = keep.tile([P, x_cols * PACK], F32, name="k_sb")
+        nc.vector.tensor_copy(
+            out=k_sb[:].rearrange("p (c j) -> p c j", j=PACK),
+            in_=k_bank[:].rearrange("p (j c) -> p c j", j=PACK),
+        )
+        q_v = q_sb[:].rearrange("p (n g j) -> p n g j", n=SAMPLES, j=PACK)
+        k_in_psum = k_bank[:].rearrange("p (j n t) -> p n t j", j=PACK, n=SAMPLES)
+        k_in_sbuf = k_sb[:].rearrange("p (n t j) -> p n t j", n=SAMPLES, j=PACK)
 
         diff_of = {}
+        d_bf_of = {}
         d_words_of = {}
         d_scales_of = {}
 
-        def subtract(chunk):
-            n, part = divmod(chunk, CHUNKS_PER_SAMPLE)
-            diff_of[chunk] = diffs.tile([P, BANK * PACK], F32, name="diff")
-            diff_v = diff_of[chunk][:].rearrange("p (g t j) -> p g t j", t=T, j=PACK)
-            for engine, lo, hi in (
-                (nc.vector, 0, VECTOR_FRAMES),
-                (nc.gpsimd, VECTOR_FRAMES, FRAMES),
-            ):
-                shape = [P, hi - lo, T, PACK]
-                first = part * FRAMES
-                engine.tensor_tensor(
-                    out=diff_v[:, lo:hi],
-                    in0=q_v[:, n, first + lo : first + hi, :].unsqueeze(2).to_broadcast(shape),
-                    in1=k_v[:, n].unsqueeze(1).to_broadcast(shape),
-                    op=ALU.subtract,
-                )
+        def make_work_tile(block):
+            work = works.tile([P, BLOCK * PACK + BLOCK * PACK // 2], F32, name="work", align_bytes=64)
+            diff_of[block] = work[:, 0 : BLOCK * PACK]
+            d_bf_of[block] = work[:, BLOCK * PACK :].bitcast(BF16)
 
-        def tanh_and_quantise(chunk):
-            d_bf = tanhs.tile([P, BANK * PACK], BF16, name="d_bf", align_bytes=64)
-            nc.scalar.activation(out=d_bf[:], in_=diff_of[chunk][:], func=ACT.Tanh)
-            d_words_of[chunk] = quantised.tile([P, BANK], U32, name="d_words", align_bytes=64)
-            d_scales_of[chunk] = quantised.tile([P, BANK], U8, name="d_scales", align_bytes=64)
-            nc.vector.quantize_mx(
-                out=d_words_of[chunk][:].bitcast(FP8X4), scales=d_scales_of[chunk][:], in_=d_bf[:]
+        def subtract(engine, k_v, block, lo, hi):
+            n, part = divmod(block, BLOCKS_PER_SAMPLE)
+            first = part * FRAMES
+            shape = [P, hi - lo, T, PACK]
+            engine.tensor_tensor(
+                out=diff_of[block][:, lo * FRAME : hi * FRAME].rearrange(
+                    "p (g t j) -> p g t j", t=T, j=PACK
+                ),
+                in0=q_v[:, n, first + lo : first + hi, :].unsqueeze(2).to_broadcast(shape),
+                in1=k_v[:, n].unsqueeze(1).to_broadcast(shape),
+                op=ALU.subtract,
             )
 
-        def make_chunk(chunk):
-            if chunk + 1 < CHUNKS:
-                subtract(chunk + 1)
-            if chunk < CHUNKS:
-                tanh_and_quantise(chunk)
+        def subtract_block(block):
+            if block < BLOCKS:
+                make_work_tile(block)
+                subtract(nc.vector, k_in_psum, block, 0, VECTOR_FRAMES)
+                subtract(nc.gpsimd, k_in_sbuf, block, VECTOR_FRAMES, FRAMES)
 
-        subtract(0)
+        def tanh(block, lo, hi):
+            nc.scalar.activation(
+                out=d_bf_of[block][:, lo * FRAME : hi * FRAME],
+                in_=diff_of[block][:, lo * FRAME : hi * FRAME],
+                func=ACT.Tanh,
+            )
+
+        def quantise(block):
+            d_words_of[block] = quantised.tile([P, BLOCK], U32, name="d_words", align_bytes=64)
+            d_scales_of[block] = quantised.tile([P, BLOCK], U8, name="d_scales", align_bytes=64)
+            nc.vector.quantize_mx(
+                out=d_words_of[block][:].bitcast(FP8X4), scales=d_scales_of[block][:], in_=d_bf_of[block]
+            )
+
+        quarter = FRAMES // 4
+        make_work_tile(0)
+        make_work_tile(1)
+        subtract(nc.gpsimd, k_in_sbuf, 1, VECTOR_FRAMES, FRAMES)
+        for i in range(4):
+            subtract(nc.vector, k_in_psum, 0, i * quarter, (i + 1) * quarter)
 
         wr_words_raw = wr_raw[:].bitcast(F32)
         wr_grouped = keep.tile([P, O * PACK], BF16, name="wr_grouped", align_bytes=64)
@@ -206,7 +234,6 @@ def tile_ta_block_pa_kernel(tc, xm, Wq, bq, Wk, bk, Wr, br, out):
             turn_rows(
                 wr_words_raw,
                 pair * H,
-                2 * PAIRS,
                 wr_grouped_words[:, pair * 2 * P * PAIRS : (pair + 1) * 2 * P * PAIRS],
                 copies[pair % 2],
             )
@@ -214,46 +241,54 @@ def tile_ta_block_pa_kernel(tc, xm, Wq, bq, Wk, bk, Wr, br, out):
         wr_scales = keep.tile([P, O], U8, name="wr_scales", align_bytes=64)
         nc.vector.quantize_mx(out=wr_words[:].bitcast(FP8X4), scales=wr_scales[:], in_=wr_grouped[:])
 
-        for chunk in range(LEAD):
-            make_chunk(chunk)
+        for i in range(4):
+            tanh(0, i * quarter, (i + 1) * quarter)
+        quantise(0)
+        subtract(nc.vector, k_in_psum, 1, 0, VECTOR_FRAMES)
+        subtract_block(2)
 
         out_v = out.rearrange("n (p a) g t -> n p a (g t)", a=O_TILES)
-        banks_done = 0
-        for group in range(CHUNKS // GROUP):
-            n, part = divmod(group * GROUP, CHUNKS_PER_SAMPLE)
+        half = FRAMES // 2
+        for block in range(BLOCKS):
+            n, part = divmod(block, BLOCKS_PER_SAMPLE)
             for a in range(O_TILES):
-                stage = stages.tile([P, GROUP * BANK], F32, name="stage")
-                for i in range(GROUP):
-                    chunk = group * GROUP + i
+                scalar_has_tanh = a in TANH_AT and block + 1 < BLOCKS
+                if scalar_has_tanh:
+                    i = TANH_AT.index(a)
+                    tanh(block + 1, i * half, (i + 1) * half)
+                if a == QUANTISE_AT and block + 1 < BLOCKS:
+                    quantise(block + 1)
+                    subtract_block(block + 3)
+
+                stage = stages.tile([P, BLOCK], F32, name="stage")
+                for i in range(BANKS_PER_BLOCK):
+                    cols = slice(i * BANK, (i + 1) * BANK)
                     bank = banks.tile([P, BANK], F32, name="bank")
                     nc.tensor.matmul_mx(
                         out=bank[:],
                         lhsT=wr_words[:, a * P : (a + 1) * P].bitcast(FP8X4),
                         lhsT_scale=wr_scales[:, a * P : (a + 1) * P],
-                        rhs=d_words_of[chunk][:].bitcast(FP8X4),
-                        rhs_scale=d_scales_of[chunk][:],
+                        rhs=d_words_of[block][:, cols].bitcast(FP8X4),
+                        rhs_scale=d_scales_of[block][:, cols],
                         start=True,
                         stop=True,
                     )
-                    if (banks_done % 8) % 3 == 0:
-                        nc.scalar.activation(
-                            out=stage[:, i * BANK : (i + 1) * BANK],
-                            in_=bank[:],
-                            func=ACT.Identity,
-                            bias=br_f32[:, a : a + 1],
-                            scale=1.0,
-                        )
-                    else:
+                    if i == 0 or scalar_has_tanh:
                         nc.vector.tensor_scalar(
-                            out=stage[:, i * BANK : (i + 1) * BANK],
+                            out=stage[:, cols],
                             in0=bank[:],
                             scalar1=br_f32[:, a : a + 1],
                             scalar2=None,
                             op0=ALU.add,
                         )
-                    banks_done += 1
+                    else:
+                        nc.scalar.activation(
+                            out=stage[:, cols],
+                            in_=bank[:],
+                            func=ACT.Identity,
+                            bias=br_f32[:, a : a + 1],
+                            scale=1.0,
+                        )
                 nc.sync.dma_start(
-                    out=out_v[n, :, a, part * BANK : (part + GROUP) * BANK], in_=stage[:]
+                    out=out_v[n, :, a, part * BLOCK : (part + 1) * BLOCK], in_=stage[:]
                 )
-                if banks_done % 8 == 0:
-                    make_chunk(LEAD + banks_done // 8 - 1)

@@ -31,6 +31,7 @@ FRAME = T * PACK
 
 VECTOR_FRAMES = 6
 TANH_AT = (1, 4)
+VECTOR_SUBTRACT_AT = 3
 QUANTISE_AT = 6
 
 FLOPS = 2 * 2 * SAMPLES * H * C * T + 2 * SAMPLES * O * H * T * T
@@ -169,7 +170,7 @@ def tile_ta_block_pa_kernel(tc, xm, Wq, bq, Wk, bk, Wr, br, out):
             op=ALU.add,
         )
         k_sb = keep.tile([P, x_cols * PACK], F32, name="k_sb")
-        nc.vector.tensor_copy(
+        nc.scalar.copy(
             out=k_sb[:].rearrange("p (c j) -> p c j", j=PACK),
             in_=k_bank[:].rearrange("p (j c) -> p c j", j=PACK),
         )
@@ -200,11 +201,14 @@ def tile_ta_block_pa_kernel(tc, xm, Wq, bq, Wk, bk, Wr, br, out):
                 op=ALU.subtract,
             )
 
-        def subtract_block(block):
+        def start_block(block):
             if block < BLOCKS:
                 make_work_tile(block)
-                subtract(nc.vector, k_in_psum, block, 0, VECTOR_FRAMES)
                 subtract(nc.gpsimd, k_in_sbuf, block, VECTOR_FRAMES, FRAMES)
+
+        def vector_share(block):
+            if block < BLOCKS:
+                subtract(nc.vector, k_in_psum, block, 0, VECTOR_FRAMES)
 
         def tanh(block, lo, hi):
             nc.scalar.activation(
@@ -222,10 +226,10 @@ def tile_ta_block_pa_kernel(tc, xm, Wq, bq, Wk, bk, Wr, br, out):
 
         quarter = FRAMES // 4
         make_work_tile(0)
-        make_work_tile(1)
-        subtract(nc.gpsimd, k_in_sbuf, 1, VECTOR_FRAMES, FRAMES)
+        start_block(1)
         for i in range(4):
             subtract(nc.vector, k_in_psum, 0, i * quarter, (i + 1) * quarter)
+        vector_share(1)
 
         wr_words_raw = wr_raw[:].bitcast(F32)
         wr_grouped = keep.tile([P, O * PACK], BF16, name="wr_grouped", align_bytes=64)
@@ -235,7 +239,7 @@ def tile_ta_block_pa_kernel(tc, xm, Wq, bq, Wk, bk, Wr, br, out):
                 wr_words_raw,
                 pair * H,
                 wr_grouped_words[:, pair * 2 * P * PAIRS : (pair + 1) * 2 * P * PAIRS],
-                copies[pair % 2],
+                nc.scalar.copy,
             )
         wr_words = keep.tile([P, O], U32, name="wr_words", align_bytes=64)
         wr_scales = keep.tile([P, O], U8, name="wr_scales", align_bytes=64)
@@ -244,8 +248,7 @@ def tile_ta_block_pa_kernel(tc, xm, Wq, bq, Wk, bk, Wr, br, out):
         for i in range(4):
             tanh(0, i * quarter, (i + 1) * quarter)
         quantise(0)
-        subtract(nc.vector, k_in_psum, 1, 0, VECTOR_FRAMES)
-        subtract_block(2)
+        start_block(2)
 
         out_v = out.rearrange("n (p a) g t -> n p a (g t)", a=O_TILES)
         half = FRAMES // 2
@@ -256,9 +259,11 @@ def tile_ta_block_pa_kernel(tc, xm, Wq, bq, Wk, bk, Wr, br, out):
                 if scalar_has_tanh:
                     i = TANH_AT.index(a)
                     tanh(block + 1, i * half, (i + 1) * half)
+                if a == VECTOR_SUBTRACT_AT:
+                    vector_share(block + 2)
                 if a == QUANTISE_AT and block + 1 < BLOCKS:
                     quantise(block + 1)
-                    subtract_block(block + 3)
+                    start_block(block + 3)
 
                 stage = stages.tile([P, BLOCK], F32, name="stage")
                 for i in range(BANKS_PER_BLOCK):

@@ -48,25 +48,6 @@ def tile_ta_block_pa_kernel(tc, xm, Wq, bq, Wk, bk, Wr, br, out):
         k_banks = ctx.enter_context(tc.psum_pool(name="k_banks", bufs=1))
         banks = ctx.enter_context(tc.psum_pool(name="banks", bufs=7))
 
-        x_raw = keep.tile([P, SAMPLES * C_PASSES * PACK * T], BF16, name="x_raw")
-        x_raw_v = x_raw[:].rearrange("p (n b et) -> p n b et", n=SAMPLES, b=C_PASSES * PAIRS)
-        for n in range(SAMPLES):
-            nc.sync.dma_start(
-                out=x_raw_v[:, n], in_=xm[n].rearrange("(b p e) t -> p b (e t)", p=P, e=2)
-            )
-
-        proj_raw = {}
-        for name, w in (("q", Wq), ("k", Wk)):
-            proj_raw[name] = keep.tile([P, H_TILES * C], BF16, name="raw_" + name)
-            for u in range(PAIRS):
-                nc.sync.dma_start(
-                    out=proj_raw[name][:, 2 * u * C : 2 * (u + 1) * C],
-                    in_=w[2 * P * u : 2 * P * (u + 1), :].rearrange("(p e) c -> p (e c)", e=2),
-                )
-
-        wr_raw = keep.tile([P, O_TILES * H], BF16, name="wr_raw")
-        nc.sync.dma_start(out=wr_raw[:], in_=Wr.rearrange("(p a) h -> p (a h)", a=O_TILES))
-
         bias_bf = {}
         for name, b in (("q", bq), ("k", bk)):
             bias_bf[name] = keep.tile([P, PACK], BF16, name="bias_" + name)
@@ -76,6 +57,31 @@ def tile_ta_block_pa_kernel(tc, xm, Wq, bq, Wk, bk, Wr, br, out):
             )
         br_bf = keep.tile([P, O_TILES], BF16, name="br_bf")
         nc.scalar.dma_start(out=br_bf[:], in_=br.rearrange("(p a) -> p a", a=O_TILES))
+
+        x_raw = keep.tile([P, SAMPLES * C_PASSES * PACK * T], BF16, name="x_raw")
+        x_raw_v = x_raw[:].rearrange("p (n b et) -> p n b et", n=SAMPLES, b=C_PASSES * PAIRS)
+
+        proj_raw = {}
+        for name, w in (("q", Wq), ("k", Wk)):
+            proj_raw[name] = keep.tile([P, H_TILES * C], BF16, name="raw_" + name)
+            for u in range(PAIRS):
+                rows = w[2 * P * u : 2 * P * (u + 1), :].rearrange("(p e) c -> p e c", e=2)
+                for e in range(2):
+                    j = 2 * u + e
+                    nc.sync.dma_start(out=proj_raw[name][:, j * C : (j + 1) * C], in_=rows[:, e])
+            if name == "q":
+                for n in range(SAMPLES):
+                    nc.sync.dma_start(
+                        out=x_raw_v[:, n], in_=xm[n].rearrange("(b p e) t -> p b (e t)", p=P, e=2)
+                    )
+
+        wr_raw = keep.tile([P, O_TILES * H], BF16, name="wr_raw")
+        wr_half = O_TILES // 2 * H
+        for i in range(2):
+            nc.sync.dma_start(
+                out=wr_raw[:, i * wr_half : (i + 1) * wr_half],
+                in_=Wr.rearrange("(p i a) h -> p i (a h)", i=2, a=O_TILES // 2)[:, i],
+            )
 
         ident = keep.tile([P, P], F32, name="ident")
         make_identity(nc, ident[:])
@@ -89,60 +95,57 @@ def tile_ta_block_pa_kernel(tc, xm, Wq, bq, Wk, bk, Wr, br, out):
             "p (g n t j) -> p g n t j", g=C_PASSES, n=SAMPLES, j=PACK
         )
         x_values = x_raw[:].rearrange("p (n g j t) -> p n g j t", n=SAMPLES, g=C_PASSES, j=PACK)
-        for n in range(SAMPLES):
-            nc.vector.tensor_copy(
-                out=x_grouped_v[:, :, n], in_=x_values[:, n].rearrange("p g j t -> p g t j")
-            )
         x_cols = SAMPLES * T
         x_words = keep.tile([P, C_PASSES * x_cols], U32, name="x_words", align_bytes=64)
         x_scales = keep.tile([P, C_PASSES * x_cols], U8, name="x_scales", align_bytes=64)
-        nc.vector.quantize_mx(out=x_words[:].bitcast(FP8X4), scales=x_scales[:], in_=x_grouped[:])
 
-        bias_qk = keep.tile([P, PACK], F32, name="bias_qk")
-        nc.vector.tensor_tensor(
-            out=bias_qk[:], in0=bias_bf["q"][:], in1=bias_bf["k"][:], op=ALU.subtract
-        )
-        br_f32 = keep.tile([P, O_TILES], F32, name="br_f32")
-        nc.vector.tensor_copy(out=br_f32[:], in_=br_bf[:])
+        def regroup_and_quantise_x():
+            for n in range(SAMPLES):
+                nc.vector.tensor_copy(
+                    out=x_grouped_v[:, :, n], in_=x_values[:, n].rearrange("p g j t -> p g t j")
+                )
+            nc.vector.quantize_mx(out=x_words[:].bitcast(FP8X4), scales=x_scales[:], in_=x_grouped[:])
 
-        def turn_rows(raw_words, first_word, grouped_words, copy):
+        def turn_rows(raw_words, first_word, blocks):
             bank = banks.tile([P, BANK], F32, name="bank")
-            for b in range(BANK // P):
+            for b in range(blocks):
                 nc.tensor.transpose(
                     bank[:, b * P : (b + 1) * P],
                     raw_words[:, first_word + b * P : first_word + (b + 1) * P],
                     ident[:],
                 )
+            return bank[:, 0 : blocks * P]
+
+        def group_words(copy, turned, grouped_words):
             copy(
                 out=grouped_words.rearrange("p (x m u) -> p x m u", m=P, u=PAIRS),
-                in_=bank[:].rearrange("p (x u m) -> p x m u", m=P, u=PAIRS),
+                in_=turned.rearrange("p (x u m) -> p x m u", m=P, u=PAIRS),
             )
 
-        copies = (nc.scalar.copy, nc.vector.tensor_copy)
-
         tile_cols = C_PASSES * P
+        grouped = {}
         proj_words = {}
         proj_scales = {}
         for name in ("q", "k"):
-            raw_words = proj_raw[name][:].bitcast(F32)
-            grouped = keep.tile([P, H_TILES * tile_cols * PACK], BF16, name="grouped_" + name, align_bytes=64)
-            grouped_words = grouped[:].bitcast(F32)
+            grouped[name] = keep.tile([P, H_TILES * tile_cols * PACK], BF16, name="grouped_" + name, align_bytes=64)
             proj_words[name] = keep.tile([P, H_TILES * tile_cols], U32, name="words_" + name, align_bytes=64)
             proj_scales[name] = keep.tile([P, H_TILES * tile_cols], U8, name="scales_" + name, align_bytes=64)
-            for u in range(PAIRS):
-                for j in (2 * u, 2 * u + 1):
-                    turn_rows(
-                        raw_words,
-                        j * (C // 2),
-                        grouped_words[:, j * tile_cols * PAIRS : (j + 1) * tile_cols * PAIRS],
-                        copies[j % 2],
-                    )
-                cols = slice(2 * u * tile_cols, 2 * (u + 1) * tile_cols)
-                nc.vector.quantize_mx(
-                    out=proj_words[name][:, cols].bitcast(FP8X4),
-                    scales=proj_scales[name][:, cols],
-                    in_=grouped[:, 2 * u * tile_cols * PACK : 2 * (u + 1) * tile_cols * PACK],
-                )
+
+        pass_words = PAIRS * P
+
+        def turn_tile(name, j, copies, first_pass, passes):
+            first = (j * C_PASSES + first_pass) * pass_words
+            turned = turn_rows(proj_raw[name][:].bitcast(F32), first, passes * PAIRS)
+            group_words(copies, turned, grouped[name][:].bitcast(F32)[:, first : first + passes * pass_words])
+
+        def quantise_tile(name, j, first_pass, passes):
+            first = (j * C_PASSES + first_pass) * P
+            cols = slice(first, first + passes * P)
+            nc.vector.quantize_mx(
+                out=proj_words[name][:, cols].bitcast(FP8X4),
+                scales=proj_scales[name][:, cols],
+                in_=grouped[name][:, first * PACK : (first + passes * P) * PACK],
+            )
 
         def project(name, bank):
             for j in range(H_TILES):
@@ -158,21 +161,42 @@ def tile_ta_block_pa_kernel(tc, xm, Wq, bq, Wk, bk, Wr, br, out):
                         stop=(g == C_PASSES - 1),
                     )
 
+        q_sb = keep.tile([P, x_cols * PACK], F32, name="q_sb")
+        k_sb = keep.tile([P, x_cols * PACK], F32, name="k_sb")
+
+        row_tiles = [(name, j) for name in ("q", "k") for j in range(H_TILES)]
+        for i, (name, j) in enumerate(row_tiles[:-1]):
+            turn_tile(name, j, nc.scalar.copy, 0, C_PASSES)
+            if i > 0:
+                quantise_tile(*row_tiles[i - 1], 0, C_PASSES)
+            if (name, j) == ("k", 0):
+                regroup_and_quantise_x()
+        bias_qk = keep.tile([P, PACK], F32, name="bias_qk")
+        nc.vector.tensor_tensor(
+            out=bias_qk[:], in0=bias_bf["q"][:], in1=bias_bf["k"][:], op=ALU.subtract
+        )
+        br_f32 = keep.tile([P, O_TILES], F32, name="br_f32")
+        nc.vector.tensor_copy(out=br_f32[:], in_=br_bf[:])
         q_bank = banks.tile([P, BANK], F32, name="bank")
         project("q", q_bank)
-        k_bank = k_banks.tile([P, BANK], F32, name="k_bank")
-        project("k", k_bank)
-        q_sb = keep.tile([P, x_cols * PACK], F32, name="q_sb")
         nc.vector.tensor_tensor(
             out=q_sb[:].rearrange("p (c j) -> p c j", j=PACK),
             in0=q_bank[:].rearrange("p (j c) -> p c j", j=PACK),
             in1=bias_qk[:].unsqueeze(1).to_broadcast([P, x_cols, PACK]),
             op=ALU.add,
         )
-        k_sb = keep.tile([P, x_cols * PACK], F32, name="k_sb")
+        quantise_tile(*row_tiles[-2], 0, C_PASSES)
+        turn_tile(*row_tiles[-1], nc.scalar.copy, 0, 1)
+        turn_tile(*row_tiles[-1], nc.vector.tensor_copy, 1, 1)
+        quantise_tile(*row_tiles[-1], 0, 1)
+        quantise_tile(*row_tiles[-1], 1, 1)
+        k_bank = k_banks.tile([P, BANK], F32, name="k_bank")
+        project("k", k_bank)
+        k_copy_bank = banks.tile([P, BANK], F32, name="bank")
+        project("k", k_copy_bank)
         nc.scalar.copy(
             out=k_sb[:].rearrange("p (c j) -> p c j", j=PACK),
-            in_=k_bank[:].rearrange("p (j c) -> p c j", j=PACK),
+            in_=k_copy_bank[:].rearrange("p (j c) -> p c j", j=PACK),
         )
         q_v = q_sb[:].rearrange("p (n g j) -> p n g j", n=SAMPLES, j=PACK)
         k_in_psum = k_bank[:].rearrange("p (j n t) -> p n t j", j=PACK, n=SAMPLES)
@@ -234,19 +258,22 @@ def tile_ta_block_pa_kernel(tc, xm, Wq, bq, Wk, bk, Wr, br, out):
         wr_words_raw = wr_raw[:].bitcast(F32)
         wr_grouped = keep.tile([P, O * PACK], BF16, name="wr_grouped", align_bytes=64)
         wr_grouped_words = wr_grouped[:].bitcast(F32)
-        for pair in range(O_TILES // 2):
-            turn_rows(
-                wr_words_raw,
-                pair * H,
-                wr_grouped_words[:, pair * 2 * P * PAIRS : (pair + 1) * 2 * P * PAIRS],
-                nc.scalar.copy,
-            )
         wr_words = keep.tile([P, O], U32, name="wr_words", align_bytes=64)
         wr_scales = keep.tile([P, O], U8, name="wr_scales", align_bytes=64)
-        nc.vector.quantize_mx(out=wr_words[:].bitcast(FP8X4), scales=wr_scales[:], in_=wr_grouped[:])
-
-        for i in range(4):
-            tanh(0, i * quarter, (i + 1) * quarter)
+        pair_cols = 2 * P
+        for pair in range(O_TILES // 2):
+            group_words(
+                nc.scalar.copy,
+                turn_rows(wr_words_raw, pair * H, BANK // P),
+                wr_grouped_words[:, pair * pair_cols * PAIRS : (pair + 1) * pair_cols * PAIRS],
+            )
+            tanh(0, pair * quarter, (pair + 1) * quarter)
+            cols = slice(pair * pair_cols, (pair + 1) * pair_cols)
+            nc.vector.quantize_mx(
+                out=wr_words[:, cols].bitcast(FP8X4),
+                scales=wr_scales[:, cols],
+                in_=wr_grouped[:, pair * pair_cols * PACK : (pair + 1) * pair_cols * PACK],
+            )
         quantise(0)
         start_block(2)
 

@@ -22,17 +22,23 @@ H_TILES = H // P
 O_TILES = O // P
 BANK = 512
 
-BANKS_PER_BLOCK = 2
-BLOCK = BANKS_PER_BLOCK * BANK
-FRAMES = BLOCK // T
-BLOCKS_PER_SAMPLE = T // FRAMES
-BLOCKS = SAMPLES * BLOCKS_PER_SAMPLE
 FRAME = T * PACK
 
-VECTOR_FRAMES = 6
-TANH_AT = (1, 4)
-VECTOR_SUBTRACT_AT = 3
-QUANTISE_AT = 6
+UNIT_FRAMES = ((8, 8, 16, 16, 16), (16, 16, 16, 16))
+UNITS = [
+    (n, sum(UNIT_FRAMES[n][:i]), frames) for n in range(SAMPLES) for i, frames in enumerate(UNIT_FRAMES[n])
+]
+MAX_FRAMES = 16
+SHORT_UNITS = 2
+
+VECTOR_FRAMES = {0: 8, 1: 8, 2: 10, 3: 10}
+VECTOR_FRAMES_LATER = 6
+
+WEAVE = {
+    16: {1: "tanh 0", 6: "tanh 1 subtract", 11: "quantise"},
+    8: {2: "tanh 0 subtract", 5: "tanh 1", 6: "quantise"},
+}
+SCALAR_SLOTS = {16: (1, 3, 5, 7, 9, 11, 13), 8: (1, 3, 5)}
 
 FLOPS = 2 * 2 * SAMPLES * H * C * T + 2 * SAMPLES * O * H * T * T
 
@@ -190,14 +196,42 @@ def tile_ta_block_pa_kernel(tc, xm, Wq, bq, Wk, bk, Wr, br, out):
         turn_tile(*row_tiles[-1], nc.vector.tensor_copy, 1, 1)
         quantise_tile(*row_tiles[-1], 0, 1)
         quantise_tile(*row_tiles[-1], 1, 1)
+
+        wr_words_raw = wr_raw[:].bitcast(F32)
+        wr_grouped = keep.tile([P, O * PACK], BF16, name="wr_grouped", align_bytes=64)
+        wr_grouped_words = wr_grouped[:].bitcast(F32)
+        wr_words = keep.tile([P, O], U32, name="wr_words", align_bytes=64)
+        wr_scales = keep.tile([P, O], U8, name="wr_scales", align_bytes=64)
+        pair_cols = 2 * P
+        wr_turned = {}
+
+        def turn_wr(pair):
+            wr_turned[pair] = turn_rows(wr_words_raw, pair * H, BANK // P)
+
+        def group_wr(pair):
+            group_words(
+                nc.scalar.copy,
+                wr_turned[pair],
+                wr_grouped_words[:, pair * pair_cols * PAIRS : (pair + 1) * pair_cols * PAIRS],
+            )
+
+        def quantise_wr(pair):
+            cols = slice(pair * pair_cols, (pair + 1) * pair_cols)
+            nc.vector.quantize_mx(
+                out=wr_words[:, cols].bitcast(FP8X4),
+                scales=wr_scales[:, cols],
+                in_=wr_grouped[:, pair * pair_cols * PACK : (pair + 1) * pair_cols * PACK],
+            )
+
+        for pair in (0, 1):
+            turn_wr(pair)
+            group_wr(pair)
+        quantise_wr(0)
+
         k_bank = k_banks.tile([P, BANK], F32, name="k_bank")
         project("k", k_bank)
         k_copy_bank = banks.tile([P, BANK], F32, name="bank")
         project("k", k_copy_bank)
-        nc.scalar.copy(
-            out=k_sb[:].rearrange("p (c j) -> p c j", j=PACK),
-            in_=k_copy_bank[:].rearrange("p (j c) -> p c j", j=PACK),
-        )
         q_v = q_sb[:].rearrange("p (n g j) -> p n g j", n=SAMPLES, j=PACK)
         k_in_psum = k_bank[:].rearrange("p (j n t) -> p n t j", j=PACK, n=SAMPLES)
         k_in_sbuf = k_sb[:].rearrange("p (n t j) -> p n t j", n=SAMPLES, j=PACK)
@@ -207,17 +241,14 @@ def tile_ta_block_pa_kernel(tc, xm, Wq, bq, Wk, bk, Wr, br, out):
         d_words_of = {}
         d_scales_of = {}
 
-        def make_work_tile(block):
-            work = works.tile([P, BLOCK * PACK + BLOCK * PACK // 2], F32, name="work", align_bytes=64)
-            diff_of[block] = work[:, 0 : BLOCK * PACK]
-            d_bf_of[block] = work[:, BLOCK * PACK :].bitcast(BF16)
+        def vector_frames(u):
+            return VECTOR_FRAMES.get(u, VECTOR_FRAMES_LATER)
 
-        def subtract(engine, k_v, block, lo, hi):
-            n, part = divmod(block, BLOCKS_PER_SAMPLE)
-            first = part * FRAMES
+        def subtract(engine, k_v, u, lo, hi):
+            n, first, frames = UNITS[u]
             shape = [P, hi - lo, T, PACK]
             engine.tensor_tensor(
-                out=diff_of[block][:, lo * FRAME : hi * FRAME].rearrange(
+                out=diff_of[u][:, lo * FRAME : hi * FRAME].rearrange(
                     "p (g t j) -> p g t j", t=T, j=PACK
                 ),
                 in0=q_v[:, n, first + lo : first + hi, :].unsqueeze(2).to_broadcast(shape),
@@ -225,95 +256,102 @@ def tile_ta_block_pa_kernel(tc, xm, Wq, bq, Wk, bk, Wr, br, out):
                 op=ALU.subtract,
             )
 
-        def start_block(block):
-            if block < BLOCKS:
-                make_work_tile(block)
-                subtract(nc.gpsimd, k_in_sbuf, block, VECTOR_FRAMES, FRAMES)
+        def start_unit(u):
+            if u >= len(UNITS):
+                return
+            work = works.tile([P, MAX_FRAMES * FRAME + MAX_FRAMES * FRAME // 2], F32, name="work", align_bytes=64)
+            diff_of[u] = work[:, 0 : MAX_FRAMES * FRAME]
+            d_bf_of[u] = work[:, MAX_FRAMES * FRAME :].bitcast(BF16)
+            if vector_frames(u) < UNITS[u][2]:
+                subtract(nc.gpsimd, k_in_sbuf, u, vector_frames(u), UNITS[u][2])
 
-        def vector_share(block):
-            if block < BLOCKS:
-                subtract(nc.vector, k_in_psum, block, 0, VECTOR_FRAMES)
+        def vector_share(u):
+            if u < len(UNITS):
+                subtract(nc.vector, k_in_psum, u, 0, vector_frames(u))
 
-        def tanh(block, lo, hi):
-            nc.scalar.activation(
-                out=d_bf_of[block][:, lo * FRAME : hi * FRAME],
-                in_=diff_of[block][:, lo * FRAME : hi * FRAME],
-                func=ACT.Tanh,
-            )
+        def tanh(u, lo, hi):
+            cols = slice(lo * FRAME, hi * FRAME)
+            nc.scalar.activation(out=d_bf_of[u][:, cols], in_=diff_of[u][:, cols], func=ACT.Tanh)
 
-        def quantise(block):
-            d_words_of[block] = quantised.tile([P, BLOCK], U32, name="d_words", align_bytes=64)
-            d_scales_of[block] = quantised.tile([P, BLOCK], U8, name="d_scales", align_bytes=64)
+        def quantise(u):
+            width = UNITS[u][2] * T
+            d_words_of[u] = quantised.tile([P, MAX_FRAMES * T], U32, name="d_words", align_bytes=64)
+            d_scales_of[u] = quantised.tile([P, MAX_FRAMES * T], U8, name="d_scales", align_bytes=64)
             nc.vector.quantize_mx(
-                out=d_words_of[block][:].bitcast(FP8X4), scales=d_scales_of[block][:], in_=d_bf_of[block]
+                out=d_words_of[u][:, 0:width].bitcast(FP8X4),
+                scales=d_scales_of[u][:, 0:width],
+                in_=d_bf_of[u][:, 0 : width * PACK],
             )
 
-        quarter = FRAMES // 4
-        make_work_tile(0)
-        start_block(1)
+        start_unit(0)
+        start_unit(1)
+        quarter = UNITS[0][2] // 4
         for i in range(4):
             subtract(nc.vector, k_in_psum, 0, i * quarter, (i + 1) * quarter)
-        vector_share(1)
+            tanh(0, i * quarter, (i + 1) * quarter)
+        quantise_wr(1)
+        half = UNITS[1][2] // 2
+        for i in range(2):
+            subtract(nc.vector, k_in_psum, 1, i * half, (i + 1) * half)
+            turn_wr(2 + i)
+            group_wr(2 + i)
+            tanh(1, i * half, (i + 1) * half)
+            if i == 0:
+                quantise(0)
 
-        wr_words_raw = wr_raw[:].bitcast(F32)
-        wr_grouped = keep.tile([P, O * PACK], BF16, name="wr_grouped", align_bytes=64)
-        wr_grouped_words = wr_grouped[:].bitcast(F32)
-        wr_words = keep.tile([P, O], U32, name="wr_words", align_bytes=64)
-        wr_scales = keep.tile([P, O], U8, name="wr_scales", align_bytes=64)
-        pair_cols = 2 * P
-        for pair in range(O_TILES // 2):
-            group_words(
-                nc.scalar.copy,
-                turn_rows(wr_words_raw, pair * H, BANK // P),
-                wr_grouped_words[:, pair * pair_cols * PAIRS : (pair + 1) * pair_cols * PAIRS],
-            )
-            tanh(0, pair * quarter, (pair + 1) * quarter)
-            cols = slice(pair * pair_cols, (pair + 1) * pair_cols)
-            nc.vector.quantize_mx(
-                out=wr_words[:, cols].bitcast(FP8X4),
-                scales=wr_scales[:, cols],
-                in_=wr_grouped[:, pair * pair_cols * PACK : (pair + 1) * pair_cols * PACK],
-            )
-        quantise(0)
-        start_block(2)
+        def weave_first(slot):
+            if slot == 2:
+                quantise_wr(2)
+            if slot == 3:
+                nc.scalar.copy(
+                    out=k_sb[:].rearrange("p (c j) -> p c j", j=PACK),
+                    in_=k_copy_bank[:].rearrange("p (j c) -> p c j", j=PACK),
+                )
+            if slot == 4:
+                quantise_wr(3)
+                quantise(1)
+                start_unit(2)
+                start_unit(3)
+                vector_share(2)
+
+        def weave(u, slot):
+            if u + 1 == len(UNITS):
+                return
+            tasks = WEAVE[UNITS[u][2]].get(slot, "")
+            if "tanh 0" in tasks:
+                tanh(u + 1, 0, vector_frames(u + 1))
+            if "tanh 1" in tasks:
+                tanh(u + 1, vector_frames(u + 1), UNITS[u + 1][2])
+            if "subtract" in tasks:
+                vector_share(u + 2)
+            if "quantise" in tasks:
+                quantise(u + 1)
+                start_unit(u + 3)
 
         out_v = out.rearrange("n (p a) g t -> n p a (g t)", a=O_TILES)
-        half = FRAMES // 2
-        for block in range(BLOCKS):
-            n, part = divmod(block, BLOCKS_PER_SAMPLE)
+        for u, (n, first, frames) in enumerate(UNITS):
+            unit_cols = frames * T
+            unit_banks = unit_cols // BANK
             for a in range(O_TILES):
-                scalar_has_tanh = a in TANH_AT and block + 1 < BLOCKS
-                if scalar_has_tanh:
-                    i = TANH_AT.index(a)
-                    tanh(block + 1, i * half, (i + 1) * half)
-                if a == VECTOR_SUBTRACT_AT:
-                    vector_share(block + 2)
-                if a == QUANTISE_AT and block + 1 < BLOCKS:
-                    quantise(block + 1)
-                    start_block(block + 3)
-
-                stage = stages.tile([P, BLOCK], F32, name="stage")
-                for i in range(BANKS_PER_BLOCK):
+                stage = stages.tile([P, MAX_FRAMES * T], F32, name="stage")
+                for i in range(unit_banks):
+                    slot = a * unit_banks + i
+                    if u == 0:
+                        weave_first(slot)
+                    else:
+                        weave(u, slot)
                     cols = slice(i * BANK, (i + 1) * BANK)
                     bank = banks.tile([P, BANK], F32, name="bank")
                     nc.tensor.matmul_mx(
                         out=bank[:],
                         lhsT=wr_words[:, a * P : (a + 1) * P].bitcast(FP8X4),
                         lhsT_scale=wr_scales[:, a * P : (a + 1) * P],
-                        rhs=d_words_of[block][:, cols].bitcast(FP8X4),
-                        rhs_scale=d_scales_of[block][:, cols],
+                        rhs=d_words_of[u][:, cols].bitcast(FP8X4),
+                        rhs_scale=d_scales_of[u][:, cols],
                         start=True,
                         stop=True,
                     )
-                    if i == 0 or scalar_has_tanh:
-                        nc.vector.tensor_scalar(
-                            out=stage[:, cols],
-                            in0=bank[:],
-                            scalar1=br_f32[:, a : a + 1],
-                            scalar2=None,
-                            op0=ALU.add,
-                        )
-                    else:
+                    if slot in SCALAR_SLOTS[frames]:
                         nc.scalar.activation(
                             out=stage[:, cols],
                             in_=bank[:],
@@ -321,6 +359,14 @@ def tile_ta_block_pa_kernel(tc, xm, Wq, bq, Wk, bk, Wr, br, out):
                             bias=br_f32[:, a : a + 1],
                             scale=1.0,
                         )
+                    else:
+                        nc.vector.tensor_scalar(
+                            out=stage[:, cols],
+                            in0=bank[:],
+                            scalar1=br_f32[:, a : a + 1],
+                            scalar2=None,
+                            op0=ALU.add,
+                        )
                 nc.sync.dma_start(
-                    out=out_v[n, :, a, part * BLOCK : (part + 1) * BLOCK], in_=stage[:]
+                    out=out_v[n, :, a, first * T : first * T + unit_cols], in_=stage[:, 0:unit_cols]
                 )

@@ -29,16 +29,20 @@ UNITS = [
     (n, sum(UNIT_FRAMES[n][:i]), frames) for n in range(SAMPLES) for i, frames in enumerate(UNIT_FRAMES[n])
 ]
 MAX_FRAMES = 16
-SHORT_UNITS = 2
 
-VECTOR_FRAMES = {0: 8, 1: 8, 2: 10, 3: 10}
+VECTOR_FRAMES = {0: 8, 1: 4, 2: 8, 3: 10}
 VECTOR_FRAMES_LATER = 6
 
 WEAVE = {
-    16: {1: "tanh 0", 6: "tanh 1 subtract", 11: "quantise"},
-    8: {2: "tanh 0 subtract", 5: "tanh 1", 6: "quantise"},
+    16: {0: ("tanh 0",), 6: ("subtract",), 8: ("tanh 1",), 12: ("quantise",)},
+    8: {2: ("tanh 0",), 3: ("subtract",), 5: ("tanh 1",), 6: ("quantise",)},
 }
 SCALAR_SLOTS = {16: (1, 3, 5, 7, 9, 11, 13), 8: (1, 3, 5)}
+
+
+def work_slot(u):
+    return "a" if u in (1, 2) or (u > 2 and u % 2 == 0) else "b"
+
 
 FLOPS = 2 * 2 * SAMPLES * H * C * T + 2 * SAMPLES * O * H * T * T
 
@@ -48,9 +52,9 @@ def tile_ta_block_pa_kernel(tc, xm, Wq, bq, Wk, bk, Wr, br, out):
     with ExitStack() as ctx:
         ctx.enter_context(tc.manual_schedule())
         keep = ctx.enter_context(tc.tile_pool(name="keep", bufs=1))
-        works = ctx.enter_context(tc.tile_pool(name="works", bufs=2))
+        works = ctx.enter_context(tc.tile_pool(name="works", bufs=1))
         quantised = ctx.enter_context(tc.tile_pool(name="quantised", bufs=3))
-        stages = ctx.enter_context(tc.tile_pool(name="stages", bufs=8))
+        stages = ctx.enter_context(tc.tile_pool(name="stages", bufs=16))
         k_banks = ctx.enter_context(tc.psum_pool(name="k_banks", bufs=1))
         banks = ctx.enter_context(tc.psum_pool(name="banks", bufs=7))
 
@@ -65,7 +69,6 @@ def tile_ta_block_pa_kernel(tc, xm, Wq, bq, Wk, bk, Wr, br, out):
         nc.scalar.dma_start(out=br_bf[:], in_=br.rearrange("(p a) -> p a", a=O_TILES))
 
         x_raw = keep.tile([P, SAMPLES * C_PASSES * PACK * T], BF16, name="x_raw")
-        x_raw_v = x_raw[:].rearrange("p (n b et) -> p n b et", n=SAMPLES, b=C_PASSES * PAIRS)
 
         proj_raw = {}
         for name, w in (("q", Wq), ("k", Wk)):
@@ -76,10 +79,10 @@ def tile_ta_block_pa_kernel(tc, xm, Wq, bq, Wk, bk, Wr, br, out):
                     j = 2 * u + e
                     nc.sync.dma_start(out=proj_raw[name][:, j * C : (j + 1) * C], in_=rows[:, e])
             if name == "q":
-                for n in range(SAMPLES):
-                    nc.sync.dma_start(
-                        out=x_raw_v[:, n], in_=xm[n].rearrange("(b p e) t -> p b (e t)", p=P, e=2)
-                    )
+                nc.sync.dma_start(
+                    out=x_raw[:].rearrange("p (b et) -> p b et", b=SAMPLES * C_PASSES * PAIRS),
+                    in_=xm.rearrange("n c t -> (n c) t").rearrange("(b p e) t -> p b (e t)", p=P, e=2),
+                )
 
         wr_raw = keep.tile([P, O_TILES * H], BF16, name="wr_raw")
         wr_half = O_TILES // 2 * H
@@ -122,8 +125,8 @@ def tile_ta_block_pa_kernel(tc, xm, Wq, bq, Wk, bk, Wr, br, out):
                 )
             return bank[:, 0 : blocks * P]
 
-        def group_words(copy, turned, grouped_words):
-            copy(
+        def group_words(turned, grouped_words):
+            nc.scalar.copy(
                 out=grouped_words.rearrange("p (x m u) -> p x m u", m=P, u=PAIRS),
                 in_=turned.rearrange("p (x u m) -> p x m u", m=P, u=PAIRS),
             )
@@ -139,10 +142,10 @@ def tile_ta_block_pa_kernel(tc, xm, Wq, bq, Wk, bk, Wr, br, out):
 
         pass_words = PAIRS * P
 
-        def turn_tile(name, j, copies, first_pass, passes):
+        def turn_tile(name, j, first_pass, passes):
             first = (j * C_PASSES + first_pass) * pass_words
             turned = turn_rows(proj_raw[name][:].bitcast(F32), first, passes * PAIRS)
-            group_words(copies, turned, grouped[name][:].bitcast(F32)[:, first : first + passes * pass_words])
+            group_words(turned, grouped[name][:].bitcast(F32)[:, first : first + passes * pass_words])
 
         def quantise_tile(name, j, first_pass, passes):
             first = (j * C_PASSES + first_pass) * P
@@ -153,8 +156,8 @@ def tile_ta_block_pa_kernel(tc, xm, Wq, bq, Wk, bk, Wr, br, out):
                 in_=grouped[name][:, first * PACK : (first + passes * P) * PACK],
             )
 
-        def project(name, bank):
-            for j in range(H_TILES):
+        def project(name, bank, tiles=range(H_TILES)):
+            for j in tiles:
                 for g in range(C_PASSES):
                     w_cols = slice((j * C_PASSES + g) * P, (j * C_PASSES + g + 1) * P)
                     nc.tensor.matmul_mx(
@@ -167,33 +170,34 @@ def tile_ta_block_pa_kernel(tc, xm, Wq, bq, Wk, bk, Wr, br, out):
                         stop=(g == C_PASSES - 1),
                     )
 
-        q_sb = keep.tile([P, x_cols * PACK], F32, name="q_sb")
-        k_sb = keep.tile([P, x_cols * PACK], F32, name="k_sb")
+        qk_sb = keep.tile([P, 2 * x_cols * PACK], F32, name="qk_sb")
+        qk_v = qk_sb[:].rearrange("p (n w t j) -> p n w t j", n=SAMPLES, w=2, j=PACK)
 
         row_tiles = [(name, j) for name in ("q", "k") for j in range(H_TILES)]
+        bias_qk = keep.tile([P, PACK], F32, name="bias_qk")
+        br_f32 = keep.tile([P, O_TILES], F32, name="br_f32")
         for i, (name, j) in enumerate(row_tiles[:-1]):
-            turn_tile(name, j, nc.scalar.copy, 0, C_PASSES)
+            turn_tile(name, j, 0, C_PASSES)
             if i > 0:
                 quantise_tile(*row_tiles[i - 1], 0, C_PASSES)
             if (name, j) == ("k", 0):
                 regroup_and_quantise_x()
-        bias_qk = keep.tile([P, PACK], F32, name="bias_qk")
-        nc.vector.tensor_tensor(
-            out=bias_qk[:], in0=bias_bf["q"][:], in1=bias_bf["k"][:], op=ALU.subtract
-        )
-        br_f32 = keep.tile([P, O_TILES], F32, name="br_f32")
-        nc.vector.tensor_copy(out=br_f32[:], in_=br_bf[:])
-        q_bank = banks.tile([P, BANK], F32, name="bank")
-        project("q", q_bank)
-        nc.vector.tensor_tensor(
-            out=q_sb[:].rearrange("p (c j) -> p c j", j=PACK),
-            in0=q_bank[:].rearrange("p (j c) -> p c j", j=PACK),
-            in1=bias_qk[:].unsqueeze(1).to_broadcast([P, x_cols, PACK]),
-            op=ALU.add,
-        )
+                nc.vector.tensor_tensor(
+                    out=bias_qk[:], in0=bias_bf["q"][:], in1=bias_bf["k"][:], op=ALU.subtract
+                )
+                nc.vector.tensor_copy(out=br_f32[:], in_=br_bf[:])
+            if (name, j) == ("k", 1):
+                q_bank = banks.tile([P, BANK], F32, name="bank")
+                project("q", q_bank)
+                nc.vector.tensor_tensor(
+                    out=qk_v[:, :, 0],
+                    in0=q_bank[:].rearrange("p (j n t) -> p n t j", j=PACK, n=SAMPLES),
+                    in1=bias_qk[:].unsqueeze(1).unsqueeze(1).to_broadcast([P, SAMPLES, T, PACK]),
+                    op=ALU.add,
+                )
+        turn_tile(*row_tiles[-1], 0, 1)
+        turn_tile(*row_tiles[-1], 1, 1)
         quantise_tile(*row_tiles[-2], 0, C_PASSES)
-        turn_tile(*row_tiles[-1], nc.scalar.copy, 0, 1)
-        turn_tile(*row_tiles[-1], nc.vector.tensor_copy, 1, 1)
         quantise_tile(*row_tiles[-1], 0, 1)
         quantise_tile(*row_tiles[-1], 1, 1)
 
@@ -210,7 +214,6 @@ def tile_ta_block_pa_kernel(tc, xm, Wq, bq, Wk, bk, Wr, br, out):
 
         def group_wr(pair):
             group_words(
-                nc.scalar.copy,
                 wr_turned[pair],
                 wr_grouped_words[:, pair * pair_cols * PAIRS : (pair + 1) * pair_cols * PAIRS],
             )
@@ -223,18 +226,24 @@ def tile_ta_block_pa_kernel(tc, xm, Wq, bq, Wk, bk, Wr, br, out):
                 in_=wr_grouped[:, pair * pair_cols * PACK : (pair + 1) * pair_cols * PACK],
             )
 
-        for pair in (0, 1):
-            turn_wr(pair)
-            group_wr(pair)
-        quantise_wr(0)
-
+        turn_wr(0)
+        group_wr(0)
         k_bank = k_banks.tile([P, BANK], F32, name="k_bank")
-        project("k", k_bank)
         k_copy_bank = banks.tile([P, BANK], F32, name="bank")
-        project("k", k_copy_bank)
-        q_v = q_sb[:].rearrange("p (n g j) -> p n g j", n=SAMPLES, j=PACK)
+        project("k", k_bank, (0, 1))
+        project("k", k_copy_bank, (0, 1))
+        turn_wr(1)
+        group_wr(1)
+        project("k", k_bank, (2, 3))
+        project("k", k_copy_bank, (2, 3))
+        quantise_wr(0)
+        nc.scalar.copy(
+            out=qk_v[:, :, 1],
+            in_=k_copy_bank[:].rearrange("p (j n t) -> p n t j", j=PACK, n=SAMPLES),
+        )
+        q_v = qk_v[:, :, 0]
         k_in_psum = k_bank[:].rearrange("p (j n t) -> p n t j", j=PACK, n=SAMPLES)
-        k_in_sbuf = k_sb[:].rearrange("p (n t j) -> p n t j", n=SAMPLES, j=PACK)
+        k_in_sbuf = qk_v[:, :, 1]
 
         diff_of = {}
         d_bf_of = {}
@@ -259,7 +268,9 @@ def tile_ta_block_pa_kernel(tc, xm, Wq, bq, Wk, bk, Wr, br, out):
         def start_unit(u):
             if u >= len(UNITS):
                 return
-            work = works.tile([P, MAX_FRAMES * FRAME + MAX_FRAMES * FRAME // 2], F32, name="work", align_bytes=64)
+            work = works.tile(
+                [P, MAX_FRAMES * FRAME + MAX_FRAMES * FRAME // 2], F32, name="work_" + work_slot(u), align_bytes=64
+            )
             diff_of[u] = work[:, 0 : MAX_FRAMES * FRAME]
             d_bf_of[u] = work[:, MAX_FRAMES * FRAME :].bitcast(BF16)
             if vector_frames(u) < UNITS[u][2]:
@@ -289,44 +300,40 @@ def tile_ta_block_pa_kernel(tc, xm, Wq, bq, Wk, bk, Wr, br, out):
         for i in range(4):
             subtract(nc.vector, k_in_psum, 0, i * quarter, (i + 1) * quarter)
             tanh(0, i * quarter, (i + 1) * quarter)
+        vector_share(1)
+        turn_wr(2)
+        group_wr(2)
+        tanh(1, 0, vector_frames(1))
+        quantise(0)
         quantise_wr(1)
-        half = UNITS[1][2] // 2
-        for i in range(2):
-            subtract(nc.vector, k_in_psum, 1, i * half, (i + 1) * half)
-            turn_wr(2 + i)
-            group_wr(2 + i)
-            tanh(1, i * half, (i + 1) * half)
-            if i == 0:
-                quantise(0)
+        quantise_wr(2)
+        turn_wr(3)
+        tanh(1, vector_frames(1), UNITS[1][2])
 
         def weave_first(slot):
-            if slot == 2:
-                quantise_wr(2)
-            if slot == 3:
-                nc.scalar.copy(
-                    out=k_sb[:].rearrange("p (c j) -> p c j", j=PACK),
-                    in_=k_copy_bank[:].rearrange("p (j c) -> p c j", j=PACK),
-                )
+            if slot == 0:
+                group_wr(3)
             if slot == 4:
                 quantise_wr(3)
                 quantise(1)
                 start_unit(2)
                 start_unit(3)
+            if slot == 5:
                 vector_share(2)
 
         def weave(u, slot):
             if u + 1 == len(UNITS):
                 return
-            tasks = WEAVE[UNITS[u][2]].get(slot, "")
-            if "tanh 0" in tasks:
-                tanh(u + 1, 0, vector_frames(u + 1))
-            if "tanh 1" in tasks:
-                tanh(u + 1, vector_frames(u + 1), UNITS[u + 1][2])
-            if "subtract" in tasks:
-                vector_share(u + 2)
-            if "quantise" in tasks:
-                quantise(u + 1)
-                start_unit(u + 3)
+            for task in WEAVE[UNITS[u][2]].get(slot, ()):
+                if task == "tanh 0":
+                    tanh(u + 1, 0, vector_frames(u + 1))
+                if task == "tanh 1":
+                    tanh(u + 1, vector_frames(u + 1), UNITS[u + 1][2])
+                if task == "subtract":
+                    vector_share(u + 2)
+                if task == "quantise":
+                    quantise(u + 1)
+                    start_unit(u + 3)
 
         out_v = out.rearrange("n (p a) g t -> n p a (g t)", a=O_TILES)
         for u, (n, first, frames) in enumerate(UNITS):

@@ -65,8 +65,6 @@ def tile_ta_block_pa_kernel(tc, xm, Wq, bq, Wk, bk, Wr, br, out):
                 out=bias_bf[name][:].rearrange("p (u e) -> p u e", e=2),
                 in_=b.rearrange("(u p e) -> p u e", p=P, e=2),
             )
-        br_bf = keep.tile([P, O_TILES], BF16, name="br_bf")
-        nc.scalar.dma_start(out=br_bf[:], in_=br.rearrange("(p a) -> p a", a=O_TILES))
 
         x_raw = keep.tile([P, SAMPLES * C_PASSES * PACK * T], BF16, name="x_raw")
 
@@ -85,12 +83,16 @@ def tile_ta_block_pa_kernel(tc, xm, Wq, bq, Wk, bk, Wr, br, out):
                 )
 
         wr_raw = keep.tile([P, O_TILES * H], BF16, name="wr_raw")
-        wr_half = O_TILES // 2 * H
+        wr_tiles = wr_raw[:].rearrange("p (a h) -> p a h", a=O_TILES)
+        wr_rows = Wr.rearrange("(a p) h -> p a h", p=P)
+        half = O_TILES // 2
         for i in range(2):
             nc.sync.dma_start(
-                out=wr_raw[:, i * wr_half : (i + 1) * wr_half],
-                in_=Wr.rearrange("(p i a) h -> p i (a h)", i=2, a=O_TILES // 2)[:, i],
+                out=wr_tiles[:, i * half : (i + 1) * half], in_=wr_rows[:, i * half : (i + 1) * half]
             )
+        br_bf = keep.tile([P, O_TILES], BF16, name="br_bf")
+        with nc.allow_non_contiguous_dma(reason="1024 single values, needed only at the end of the head"):
+            nc.sync.dma_start(out=br_bf[:], in_=br.rearrange("(a p) -> p a", p=P))
 
         ident = keep.tile([P, P], F32, name="ident")
         make_identity(nc, ident[:])
@@ -185,7 +187,6 @@ def tile_ta_block_pa_kernel(tc, xm, Wq, bq, Wk, bk, Wr, br, out):
                 nc.vector.tensor_tensor(
                     out=bias_qk[:], in0=bias_bf["q"][:], in1=bias_bf["k"][:], op=ALU.subtract
                 )
-                nc.vector.tensor_copy(out=br_f32[:], in_=br_bf[:])
             if (name, j) == ("k", 1):
                 q_bank = banks.tile([P, BANK], F32, name="bank")
                 project("q", q_bank)
@@ -307,6 +308,7 @@ def tile_ta_block_pa_kernel(tc, xm, Wq, bq, Wk, bk, Wr, br, out):
         quantise(0)
         quantise_wr(1)
         quantise_wr(2)
+        nc.vector.tensor_copy(out=br_f32[:], in_=br_bf[:])
         turn_wr(3)
         tanh(1, vector_frames(1), UNITS[1][2])
 
@@ -335,7 +337,7 @@ def tile_ta_block_pa_kernel(tc, xm, Wq, bq, Wk, bk, Wr, br, out):
                     quantise(u + 1)
                     start_unit(u + 3)
 
-        out_v = out.rearrange("n (p a) g t -> n p a (g t)", a=O_TILES)
+        out_v = out.rearrange("n (a p) g t -> n p a (g t)", p=P)
         for u, (n, first, frames) in enumerate(UNITS):
             unit_cols = frames * T
             unit_banks = unit_cols // BANK

@@ -35,9 +35,10 @@ VECTOR_FRAMES_LATER = 6
 
 WEAVE = {
     16: {0: ("tanh 0",), 6: ("subtract",), 8: ("tanh 1",), 12: ("quantise",)},
-    8: {2: ("tanh 0",), 3: ("subtract",), 5: ("tanh 1",), 6: ("quantise",)},
+    8: {2: ("tanh 0",), 3: ("subtract", "tanh 1"), 6: ("quantise",)},
 }
-SCALAR_SLOTS = {16: (1, 3, 5, 7, 9, 11, 13), 8: (1, 3, 5)}
+SCALAR_SLOTS = {16: (3, 5, 7, 9, 11, 13, 15), 8: (1, 3, 5)}
+SCALAR_SLOTS_FIRST = (2, 4, 6)
 
 
 def work_slot(u):
@@ -360,7 +361,7 @@ def tile_ta_block_pa_kernel(tc, xm, Wq, bq, Wk, bk, Wr, br, out):
                         start=True,
                         stop=True,
                     )
-                    if slot in SCALAR_SLOTS[frames]:
+                    if slot in (SCALAR_SLOTS[frames] if u > 0 else SCALAR_SLOTS_FIRST):
                         nc.scalar.activation(
                             out=stage[:, cols],
                             in_=bank[:],

@@ -30,15 +30,31 @@ UNITS = [
 ]
 MAX_FRAMES = 16
 
-VECTOR_FRAMES = {0: 8, 1: 4, 2: 8, 3: 10}
-VECTOR_FRAMES_LATER = 6
+VECTOR_FRAMES = {0: 8, 1: 4, 2: 8, 3: 4}
+VECTOR_FRAMES_LATER = 2
+TENSOR_FRAMES = 4
+PAIR = 2
+TENSOR_PAIRS = TENSOR_FRAMES // PAIR
+BLOCKS_OF_16 = T // MAX_FRAMES
 
 WEAVE = {
-    16: {0: ("tanh 0",), 6: ("subtract",), 8: ("tanh 1",), 12: ("quantise",)},
-    8: {2: ("tanh 0",), 3: ("subtract", "tanh 1"), 6: ("quantise",)},
+    16: {
+        0: ("pair 0", "pair 1", "tanh vector", "tanh gpsimd"),
+        6: ("subtract",),
+        7: ("tanh 0",),
+        9: ("tanh 1",),
+        12: ("quantise",),
+    },
+    8: {
+        0: ("pair 0",),
+        1: ("pair 1", "tanh 0"),
+        2: ("tanh vector", "tanh 1"),
+        3: ("subtract", "tanh gpsimd"),
+        6: ("quantise",),
+    },
 }
-SCALAR_SLOTS = {16: (3, 5, 7, 9, 11, 13, 15), 8: (1, 3, 5)}
-SCALAR_SLOTS_FIRST = (2, 4, 6)
+SCALAR_SLOTS = {16: (3, 5, 11, 13, 15), 8: (4, 6)}
+SCALAR_SLOTS_FIRST = (2, 4, 5, 6)
 
 
 def work_slot(u):
@@ -55,7 +71,7 @@ def tile_ta_block_pa_kernel(tc, xm, Wq, bq, Wk, bk, Wr, br, out):
         keep = ctx.enter_context(tc.tile_pool(name="keep", bufs=1))
         works = ctx.enter_context(tc.tile_pool(name="works", bufs=1))
         quantised = ctx.enter_context(tc.tile_pool(name="quantised", bufs=3))
-        stages = ctx.enter_context(tc.tile_pool(name="stages", bufs=16))
+        stages = ctx.enter_context(tc.tile_pool(name="stages", bufs=8))
         k_banks = ctx.enter_context(tc.psum_pool(name="k_banks", bufs=1))
         banks = ctx.enter_context(tc.psum_pool(name="banks", bufs=7))
 
@@ -97,6 +113,16 @@ def tile_ta_block_pa_kernel(tc, xm, Wq, bq, Wk, bk, Wr, br, out):
 
         ident = keep.tile([P, P], F32, name="ident")
         make_identity(nc, ident[:])
+
+        choice = keep.tile([P, BLOCKS_OF_16 * TENSOR_FRAMES * T], F32, name="choice")
+        choice_shape = [P, BLOCKS_OF_16, TENSOR_FRAMES, T]
+        query_rows = ident[:, 0:T].rearrange("p (b f) -> p b f", b=BLOCKS_OF_16)
+        nc.gpsimd.tensor_tensor(
+            out=choice[:].rearrange("p (b f t) -> p b f t", b=BLOCKS_OF_16, t=T),
+            in0=query_rows[:, :, MAX_FRAMES - TENSOR_FRAMES :].unsqueeze(3).to_broadcast(choice_shape),
+            in1=ident[:, T:P].unsqueeze(1).unsqueeze(1).to_broadcast(choice_shape),
+            op=ALU.subtract,
+        )
 
         warm = keep.tile([P, 2], F32, name="warm")
         nc.vector.memset(warm[:], 0.0)
@@ -247,13 +273,50 @@ def tile_ta_block_pa_kernel(tc, xm, Wq, bq, Wk, bk, Wr, br, out):
         k_in_psum = k_bank[:].rearrange("p (j n t) -> p n t j", j=PACK, n=SAMPLES)
         k_in_sbuf = qk_v[:, :, 1]
 
+        qk_turned = {}
+
+        def turn_qk(n):
+            bank = banks.tile([P, BANK], F32, name="bank")
+            sources = qk_sb[:].rearrange("p (n c j) -> p n j c", n=SAMPLES, j=PACK)
+            for j in range(PACK):
+                nc.tensor.transpose(bank[:, j * P : (j + 1) * P], sources[:, n, j], ident[:])
+            qk_turned[n] = keep.tile([P, BANK], F32, name="qk_turned_" + str(n))
+            nc.scalar.copy(out=qk_turned[n][:], in_=bank[:])
+
         diff_of = {}
+        pair_of = {}
         d_bf_of = {}
         d_words_of = {}
         d_scales_of = {}
 
         def vector_frames(u):
             return VECTOR_FRAMES.get(u, VECTOR_FRAMES_LATER)
+
+        def gpsimd_end(u):
+            frames = UNITS[u][2]
+            return frames - TENSOR_FRAMES if frames == MAX_FRAMES else frames
+
+        def tensor_pair(u, i):
+            n, first, frames = UNITS[u]
+            lo = (first // MAX_FRAMES * TENSOR_FRAMES + i * PAIR) * T
+            bank = banks.tile([P, BANK], F32, name="bank")
+            for j in range(PACK):
+                nc.tensor.matmul(
+                    out=bank[:, j * P : (j + 1) * P],
+                    lhsT=qk_turned[n][:, j * P : (j + 1) * P],
+                    rhs=choice[:, lo : lo + PAIR * T],
+                    start=True,
+                    stop=True,
+                )
+            pair_of[u, i] = bank
+
+        def tanh_pair(u, i):
+            lo = gpsimd_end(u) + i * PAIR
+            nc.scalar.activation(
+                out=d_bf_of[u][:, lo * FRAME : (lo + PAIR) * FRAME].rearrange("p (c j) -> p c j", j=PACK),
+                in_=pair_of[u, i][:].rearrange("p (j c) -> p c j", j=PACK),
+                func=ACT.Tanh,
+            )
 
         def subtract(engine, k_v, u, lo, hi):
             n, first, frames = UNITS[u]
@@ -275,8 +338,8 @@ def tile_ta_block_pa_kernel(tc, xm, Wq, bq, Wk, bk, Wr, br, out):
             )
             diff_of[u] = work[:, 0 : MAX_FRAMES * FRAME]
             d_bf_of[u] = work[:, MAX_FRAMES * FRAME :].bitcast(BF16)
-            if vector_frames(u) < UNITS[u][2]:
-                subtract(nc.gpsimd, k_in_sbuf, u, vector_frames(u), UNITS[u][2])
+            if vector_frames(u) < gpsimd_end(u):
+                subtract(nc.gpsimd, k_in_sbuf, u, vector_frames(u), gpsimd_end(u))
 
         def vector_share(u):
             if u < len(UNITS):
@@ -314,27 +377,34 @@ def tile_ta_block_pa_kernel(tc, xm, Wq, bq, Wk, bk, Wr, br, out):
         tanh(1, vector_frames(1), UNITS[1][2])
 
         def weave_first(slot):
-            if slot == 0:
+            if slot == 2:
                 group_wr(3)
             if slot == 4:
+                turn_qk(0)
                 quantise_wr(3)
                 quantise(1)
                 start_unit(2)
                 start_unit(3)
-            if slot == 5:
                 vector_share(2)
 
         def weave(u, slot):
             if u + 1 == len(UNITS):
                 return
+            if (u, slot) == (3, 2):
+                turn_qk(1)
             for task in WEAVE[UNITS[u][2]].get(slot, ()):
-                if task == "tanh 0":
+                what, part = task.split(" ") if " " in task else (task, "")
+                if what == "pair":
+                    tensor_pair(u + 1, int(part))
+                elif part == "vector":
                     tanh(u + 1, 0, vector_frames(u + 1))
-                if task == "tanh 1":
-                    tanh(u + 1, vector_frames(u + 1), UNITS[u + 1][2])
-                if task == "subtract":
+                elif part == "gpsimd":
+                    tanh(u + 1, vector_frames(u + 1), gpsimd_end(u + 1))
+                elif what == "tanh":
+                    tanh_pair(u + 1, int(part))
+                elif what == "subtract":
                     vector_share(u + 2)
-                if task == "quantise":
+                else:
                     quantise(u + 1)
                     start_unit(u + 3)
 
@@ -343,7 +413,9 @@ def tile_ta_block_pa_kernel(tc, xm, Wq, bq, Wk, bk, Wr, br, out):
             unit_cols = frames * T
             unit_banks = unit_cols // BANK
             for a in range(O_TILES):
-                stage = stages.tile([P, MAX_FRAMES * T], F32, name="stage")
+                tiles = 1 if u < 3 else 2
+                if a % tiles == 0:
+                    stage = stages.tile([P, 2 * MAX_FRAMES * T], F32, name="stage")
                 for i in range(unit_banks):
                     slot = a * unit_banks + i
                     if u == 0:
@@ -351,6 +423,8 @@ def tile_ta_block_pa_kernel(tc, xm, Wq, bq, Wk, bk, Wr, br, out):
                     else:
                         weave(u, slot)
                     cols = slice(i * BANK, (i + 1) * BANK)
+                    place = a % tiles * unit_cols + i * BANK
+                    stage_cols = slice(place, place + BANK)
                     bank = banks.tile([P, BANK], F32, name="bank")
                     nc.tensor.matmul_mx(
                         out=bank[:],
@@ -363,7 +437,7 @@ def tile_ta_block_pa_kernel(tc, xm, Wq, bq, Wk, bk, Wr, br, out):
                     )
                     if slot in (SCALAR_SLOTS[frames] if u > 0 else SCALAR_SLOTS_FIRST):
                         nc.scalar.activation(
-                            out=stage[:, cols],
+                            out=stage[:, stage_cols],
                             in_=bank[:],
                             func=ACT.Identity,
                             bias=br_f32[:, a : a + 1],
@@ -371,12 +445,14 @@ def tile_ta_block_pa_kernel(tc, xm, Wq, bq, Wk, bk, Wr, br, out):
                         )
                     else:
                         nc.vector.tensor_scalar(
-                            out=stage[:, cols],
+                            out=stage[:, stage_cols],
                             in0=bank[:],
                             scalar1=br_f32[:, a : a + 1],
                             scalar2=None,
                             op0=ALU.add,
                         )
-                nc.sync.dma_start(
-                    out=out_v[n, :, a, first * T : first * T + unit_cols], in_=stage[:, 0:unit_cols]
-                )
+                if a % tiles == tiles - 1:
+                    nc.sync.dma_start(
+                        out=out_v[n, :, a + 1 - tiles : a + 1, first * T : first * T + unit_cols],
+                        in_=stage[:, 0 : tiles * unit_cols].rearrange("p (a c) -> p a c", a=tiles),
+                    )

from contextlib import ExitStack

import concourse.mybir as mybir
from concourse.masks import make_identity

F32 = mybir.dt.float32
BF16 = mybir.dt.bfloat16
U32 = mybir.dt.uint32
U8 = mybir.dt.uint8
FP8X4 = mybir.dt.float8_e4m3fn_x4
ALU = mybir.AluOpType
ACT = mybir.ActivationFunctionType

SAMPLES, C, T, H, O = 2, 1024, 64, 512, 1024

P = 128
PACK = 4
PAIRS = 2
K_PASS = P * PACK
C_PASSES = C // K_PASS
H_TILES = H // P
O_TILES = O // P
BANK = 512

FRAME = T * PACK

UNIT_FRAMES = ((8, 8, 16, 16, 16), (16, 16, 16, 16))
UNITS = [
    (n, sum(UNIT_FRAMES[n][:i]), frames) for n in range(SAMPLES) for i, frames in enumerate(UNIT_FRAMES[n])
]
MAX_FRAMES = 16

VECTOR_FRAMES = {0: 8, 1: 4, 2: 8, 3: 4}
VECTOR_FRAMES_LATER = 2
TENSOR_FRAMES = 4
PAIR = 2
TENSOR_PAIRS = TENSOR_FRAMES // PAIR
BLOCKS_OF_16 = T // MAX_FRAMES

WEAVE = {
    16: {
        0: ("pair 0", "pair 1", "tanh vector", "tanh gpsimd"),
        6: ("subtract",),
        7: ("tanh 0",),
        9: ("tanh 1",),
        12: ("quantise",),
    },
    8: {
        0: ("pair 0",),
        1: ("pair 1", "tanh 0"),
        2: ("tanh vector", "tanh 1"),
        3: ("subtract", "tanh gpsimd"),
        6: ("quantise",),
    },
}
SCALAR_SLOTS = {16: (3, 5, 11, 13, 15), 8: (4, 6)}
SCALAR_SLOTS_FIRST = (2, 4, 5, 6)


def work_slot(u):
    return "a" if u in (1, 2) or (u > 2 and u % 2 == 0) else "b"


FLOPS = 2 * 2 * SAMPLES * H * C * T + 2 * SAMPLES * O * H * T * T


def tile_ta_block_pa_kernel(tc, xm, Wq, bq, Wk, bk, Wr, br, out):
    nc = tc.nc
    with ExitStack() as ctx:
        ctx.enter_context(tc.manual_schedule())
        keep = ctx.enter_context(tc.tile_pool(name="keep", bufs=1))
        works = ctx.enter_context(tc.tile_pool(name="works", bufs=1))
        quantised = ctx.enter_context(tc.tile_pool(name="quantised", bufs=3))
        stages = ctx.enter_context(tc.tile_pool(name="stages", bufs=8))
        k_banks = ctx.enter_context(tc.psum_pool(name="k_banks", bufs=1))
        banks = ctx.enter_context(tc.psum_pool(name="banks", bufs=7))

        bias_bf = {}
        for name, b in (("q", bq), ("k", bk)):
            bias_bf[name] = keep.tile([P, PACK], BF16, name="bias_" + name)
            nc.scalar.dma_start(
                out=bias_bf[name][:].rearrange("p (u e) -> p u e", e=2),
                in_=b.rearrange("(u p e) -> p u e", p=P, e=2),
            )

        x_raw = keep.tile([P, SAMPLES * C_PASSES * PACK * T], BF16, name="x_raw")

        proj_raw = {}
        for name, w in (("q", Wq), ("k", Wk)):
            proj_raw[name] = keep.tile([P, H_TILES * C], BF16, name="raw_" + name)
            for u in range(PAIRS):
                rows = w[2 * P * u : 2 * P * (u + 1), :].rearrange("(p e) c -> p e c", e=2)
                for e in range(2):
                    j = 2 * u + e
                    nc.sync.dma_start(out=proj_raw[name][:, j * C : (j + 1) * C], in_=rows[:, e])
            if name == "q":
                nc.sync.dma_start(
                    out=x_raw[:].rearrange("p (b et) -> p b et", b=SAMPLES * C_PASSES * PAIRS),
                    in_=xm.rearrange("n c t -> (n c) t").rearrange("(b p e) t -> p b (e t)", p=P, e=2),
                )

        wr_raw = keep.tile([P, O_TILES * H], BF16, name="wr_raw")
        wr_tiles = wr_raw[:].rearrange("p (a h) -> p a h", a=O_TILES)
        wr_rows = Wr.rearrange("(a p) h -> p a h", p=P)
        half = O_TILES // 2
        for i in range(2):
            nc.sync.dma_start(
                out=wr_tiles[:, i * half : (i + 1) * half], in_=wr_rows[:, i * half : (i + 1) * half]
            )
        br_bf = keep.tile([P, O_TILES], BF16, name="br_bf")
        with nc.allow_non_contiguous_dma(reason="1024 single values, needed only at the end of the head"):
            nc.sync.dma_start(out=br_bf[:], in_=br.rearrange("(a p) -> p a", p=P))

        ident = keep.tile([P, P], F32, name="ident")
        make_identity(nc, ident[:])

        choice = keep.tile([P, BLOCKS_OF_16 * TENSOR_FRAMES * T], F32, name="choice")
        choice_shape = [P, BLOCKS_OF_16, TENSOR_FRAMES, T]
        query_rows = ident[:, 0:T].rearrange("p (b f) -> p b f", b=BLOCKS_OF_16)
        nc.gpsimd.tensor_tensor(
            out=choice[:].rearrange("p (b f t) -> p b f t", b=BLOCKS_OF_16, t=T),
            in0=query_rows[:, :, MAX_FRAMES - TENSOR_FRAMES :].unsqueeze(3).to_broadcast(choice_shape),
            in1=ident[:, T:P].unsqueeze(1).unsqueeze(1).to_broadcast(choice_shape),
            op=ALU.subtract,
        )

        warm = keep.tile([P, 2], F32, name="warm")
        nc.vector.memset(warm[:], 0.0)
        nc.scalar.activation(out=warm[:, 1:2], in_=warm[:, 0:1], func=ACT.Tanh)

        x_grouped = keep.tile([P, C_PASSES * SAMPLES * T * PACK], BF16, name="x_grouped", align_bytes=64)
        x_grouped_v = x_grouped[:].rearrange(
            "p (g n t j) -> p g n t j", g=C_PASSES, n=SAMPLES, j=PACK
        )
        x_values = x_raw[:].rearrange("p (n g j t) -> p n g j t", n=SAMPLES, g=C_PASSES, j=PACK)
        x_cols = SAMPLES * T
        x_words = keep.tile([P, C_PASSES * x_cols], U32, name="x_words", align_bytes=64)
        x_scales = keep.tile([P, C_PASSES * x_cols], U8, name="x_scales", align_bytes=64)

        def regroup_and_quantise_x():
            for n in range(SAMPLES):
                nc.vector.tensor_copy(
                    out=x_grouped_v[:, :, n], in_=x_values[:, n].rearrange("p g j t -> p g t j")
                )
            nc.vector.quantize_mx(out=x_words[:].bitcast(FP8X4), scales=x_scales[:], in_=x_grouped[:])

        def turn_rows(raw_words, first_word, blocks):
            bank = banks.tile([P, BANK], F32, name="bank")
            for b in range(blocks):
                nc.tensor.transpose(
                    bank[:, b * P : (b + 1) * P],
                    raw_words[:, first_word + b * P : first_word + (b + 1) * P],
                    ident[:],
                )
            return bank[:, 0 : blocks * P]

        def group_words(turned, grouped_words):
            nc.scalar.copy(
                out=grouped_words.rearrange("p (x m u) -> p x m u", m=P, u=PAIRS),
                in_=turned.rearrange("p (x u m) -> p x m u", m=P, u=PAIRS),
            )

        tile_cols = C_PASSES * P
        grouped = {}
        proj_words = {}
        proj_scales = {}
        for name in ("q", "k"):
            grouped[name] = keep.tile([P, H_TILES * tile_cols * PACK], BF16, name="grouped_" + name, align_bytes=64)
            proj_words[name] = keep.tile([P, H_TILES * tile_cols], U32, name="words_" + name, align_bytes=64)
            proj_scales[name] = keep.tile([P, H_TILES * tile_cols], U8, name="scales_" + name, align_bytes=64)

        pass_words = PAIRS * P

        def turn_tile(name, j, first_pass, passes):
            first = (j * C_PASSES + first_pass) * pass_words
            turned = turn_rows(proj_raw[name][:].bitcast(F32), first, passes * PAIRS)
            group_words(turned, grouped[name][:].bitcast(F32)[:, first : first + passes * pass_words])

        def quantise_tile(name, j, first_pass, passes):
            first = (j * C_PASSES + first_pass) * P
            cols = slice(first, first + passes * P)
            nc.vector.quantize_mx(
                out=proj_words[name][:, cols].bitcast(FP8X4),
                scales=proj_scales[name][:, cols],
                in_=grouped[name][:, first * PACK : (first + passes * P) * PACK],
            )

        def project(name, bank, tiles=range(H_TILES)):
            for j in tiles:
                for g in range(C_PASSES):
                    w_cols = slice((j * C_PASSES + g) * P, (j * C_PASSES + g + 1) * P)
                    nc.tensor.matmul_mx(
                        out=bank[:, j * x_cols : (j + 1) * x_cols],
                        lhsT=proj_words[name][:, w_cols].bitcast(FP8X4),
                        lhsT_scale=proj_scales[name][:, w_cols],
                        rhs=x_words[:, g * x_cols : (g + 1) * x_cols].bitcast(FP8X4),
                        rhs_scale=x_scales[:, g * x_cols : (g + 1) * x_cols],
                        start=(g == 0),
                        stop=(g == C_PASSES - 1),
                    )

        qk_sb = keep.tile([P, 2 * x_cols * PACK], F32, name="qk_sb")
        qk_v = qk_sb[:].rearrange("p (n w t j) -> p n w t j", n=SAMPLES, w=2, j=PACK)

        row_tiles = [(name, j) for name in ("q", "k") for j in range(H_TILES)]
        bias_qk = keep.tile([P, PACK], F32, name="bias_qk")
        br_f32 = keep.tile([P, O_TILES], F32, name="br_f32")
        for i, (name, j) in enumerate(row_tiles[:-1]):
            turn_tile(name, j, 0, C_PASSES)
            if i > 0:
                quantise_tile(*row_tiles[i - 1], 0, C_PASSES)
            if (name, j) == ("k", 0):
                regroup_and_quantise_x()
                nc.vector.tensor_tensor(
                    out=bias_qk[:], in0=bias_bf["q"][:], in1=bias_bf["k"][:], op=ALU.subtract
                )
            if (name, j) == ("k", 1):
                q_bank = banks.tile([P, BANK], F32, name="bank")
                project("q", q_bank)
                nc.vector.tensor_tensor(
                    out=qk_v[:, :, 0],
                    in0=q_bank[:].rearrange("p (j n t) -> p n t j", j=PACK, n=SAMPLES),
                    in1=bias_qk[:].unsqueeze(1).unsqueeze(1).to_broadcast([P, SAMPLES, T, PACK]),
                    op=ALU.add,
                )
        turn_tile(*row_tiles[-1], 0, 1)
        turn_tile(*row_tiles[-1], 1, 1)
        quantise_tile(*row_tiles[-2], 0, C_PASSES)
        quantise_tile(*row_tiles[-1], 0, 1)
        quantise_tile(*row_tiles[-1], 1, 1)

        wr_words_raw = wr_raw[:].bitcast(F32)
        wr_grouped = keep.tile([P, O * PACK], BF16, name="wr_grouped", align_bytes=64)
        wr_grouped_words = wr_grouped[:].bitcast(F32)
        wr_words = keep.tile([P, O], U32, name="wr_words", align_bytes=64)
        wr_scales = keep.tile([P, O], U8, name="wr_scales", align_bytes=64)
        pair_cols = 2 * P
        wr_turned = {}

        def turn_wr(pair):
            wr_turned[pair] = turn_rows(wr_words_raw, pair * H, BANK // P)

        def group_wr(pair):
            group_words(
                wr_turned[pair],
                wr_grouped_words[:, pair * pair_cols * PAIRS : (pair + 1) * pair_cols * PAIRS],
            )

        def quantise_wr(pair):
            cols = slice(pair * pair_cols, (pair + 1) * pair_cols)
            nc.vector.quantize_mx(
                out=wr_words[:, cols].bitcast(FP8X4),
                scales=wr_scales[:, cols],
                in_=wr_grouped[:, pair * pair_cols * PACK : (pair + 1) * pair_cols * PACK],
            )

        turn_wr(0)
        group_wr(0)
        k_bank = k_banks.tile([P, BANK], F32, name="k_bank")
        k_copy_bank = banks.tile([P, BANK], F32, name="bank")
        project("k", k_bank, (0, 1))
        project("k", k_copy_bank, (0, 1))
        turn_wr(1)
        group_wr(1)
        project("k", k_bank, (2, 3))
        project("k", k_copy_bank, (2, 3))
        quantise_wr(0)
        nc.scalar.copy(
            out=qk_v[:, :, 1],
            in_=k_copy_bank[:].rearrange("p (j n t) -> p n t j", j=PACK, n=SAMPLES),
        )
        q_v = qk_v[:, :, 0]
        k_in_psum = k_bank[:].rearrange("p (j n t) -> p n t j", j=PACK, n=SAMPLES)
        k_in_sbuf = qk_v[:, :, 1]

        qk_turned = {}

        def turn_qk(n):
            bank = banks.tile([P, BANK], F32, name="bank")
            sources = qk_sb[:].rearrange("p (n c j) -> p n j c", n=SAMPLES, j=PACK)
            for j in range(PACK):
                nc.tensor.transpose(bank[:, j * P : (j + 1) * P], sources[:, n, j], ident[:])
            qk_turned[n] = keep.tile([P, BANK], F32, name="qk_turned_" + str(n))
            nc.scalar.copy(out=qk_turned[n][:], in_=bank[:])

        diff_of = {}
        pair_of = {}
        d_bf_of = {}
        d_words_of = {}
        d_scales_of = {}

        def vector_frames(u):
            return VECTOR_FRAMES.get(u, VECTOR_FRAMES_LATER)

        def gpsimd_end(u):
            frames = UNITS[u][2]
            return frames - TENSOR_FRAMES if frames == MAX_FRAMES else frames

        def tensor_pair(u, i):
            n, first, frames = UNITS[u]
            lo = (first // MAX_FRAMES * TENSOR_FRAMES + i * PAIR) * T
            bank = banks.tile([P, BANK], F32, name="bank")
            for j in range(PACK):
                nc.tensor.matmul(
                    out=bank[:, j * P : (j + 1) * P],
                    lhsT=qk_turned[n][:, j * P : (j + 1) * P],
                    rhs=choice[:, lo : lo + PAIR * T],
                    start=True,
                    stop=True,
                )
            pair_of[u, i] = bank

        def tanh_pair(u, i):
            lo = gpsimd_end(u) + i * PAIR
            nc.scalar.activation(
                out=d_bf_of[u][:, lo * FRAME : (lo + PAIR) * FRAME].rearrange("p (c j) -> p c j", j=PACK),
                in_=pair_of[u, i][:].rearrange("p (j c) -> p c j", j=PACK),
                func=ACT.Tanh,
            )

        def subtract(engine, k_v, u, lo, hi):
            n, first, frames = UNITS[u]
            shape = [P, hi - lo, T, PACK]
            engine.tensor_tensor(
                out=diff_of[u][:, lo * FRAME : hi * FRAME].rearrange(
                    "p (g t j) -> p g t j", t=T, j=PACK
                ),
                in0=q_v[:, n, first + lo : first + hi, :].unsqueeze(2).to_broadcast(shape),
                in1=k_v[:, n].unsqueeze(1).to_broadcast(shape),
                op=ALU.subtract,
            )

        def start_unit(u):
            if u >= len(UNITS):
                return
            work = works.tile(
                [P, MAX_FRAMES * FRAME + MAX_FRAMES * FRAME // 2], F32, name="work_" + work_slot(u), align_bytes=64
            )
            diff_of[u] = work[:, 0 : MAX_FRAMES * FRAME]
            d_bf_of[u] = work[:, MAX_FRAMES * FRAME :].bitcast(BF16)
            if vector_frames(u) < gpsimd_end(u):
                subtract(nc.gpsimd, k_in_sbuf, u, vector_frames(u), gpsimd_end(u))

        def vector_share(u):
            if u < len(UNITS):
                subtract(nc.vector, k_in_psum, u, 0, vector_frames(u))

        def tanh(u, lo, hi):
            cols = slice(lo * FRAME, hi * FRAME)
            nc.scalar.activation(out=d_bf_of[u][:, cols], in_=diff_of[u][:, cols], func=ACT.Tanh)

        def quantise(u):
            width = UNITS[u][2] * T
            d_words_of[u] = quantised.tile([P, MAX_FRAMES * T], U32, name="d_words", align_bytes=64)
            d_scales_of[u] = quantised.tile([P, MAX_FRAMES * T], U8, name="d_scales", align_bytes=64)
            nc.vector.quantize_mx(
                out=d_words_of[u][:, 0:width].bitcast(FP8X4),
                scales=d_scales_of[u][:, 0:width],
                in_=d_bf_of[u][:, 0 : width * PACK],
            )

        start_unit(0)
        start_unit(1)
        quarter = UNITS[0][2] // 4
        for i in range(4):
            subtract(nc.vector, k_in_psum, 0, i * quarter, (i + 1) * quarter)
            tanh(0, i * quarter, (i + 1) * quarter)
        vector_share(1)
        turn_wr(2)
        group_wr(2)
        tanh(1, 0, vector_frames(1))
        quantise(0)
        quantise_wr(1)
        quantise_wr(2)
        nc.vector.tensor_copy(out=br_f32[:], in_=br_bf[:])
        turn_wr(3)
        tanh(1, vector_frames(1), UNITS[1][2])

        def weave_first(slot):
            if slot == 2:
                group_wr(3)
            if slot == 4:
                turn_qk(0)
                quantise_wr(3)
                quantise(1)
                start_unit(2)
                start_unit(3)
                vector_share(2)

        def weave(u, slot):
            if u + 1 == len(UNITS):
                return
            if (u, slot) == (3, 2):
                turn_qk(1)
            for task in WEAVE[UNITS[u][2]].get(slot, ()):
                what, part = task.split(" ") if " " in task else (task, "")
                if what == "pair":
                    tensor_pair(u + 1, int(part))
                elif part == "vector":
                    tanh(u + 1, 0, vector_frames(u + 1))
                elif part == "gpsimd":
                    tanh(u + 1, vector_frames(u + 1), gpsimd_end(u + 1))
                elif what == "tanh":
                    tanh_pair(u + 1, int(part))
                elif what == "subtract":
                    vector_share(u + 2)
                else:
                    quantise(u + 1)
                    start_unit(u + 3)

        out_v = out.rearrange("n (a p) g t -> n p a (g t)", p=P)
        for u, (n, first, frames) in enumerate(UNITS):
            unit_cols = frames * T
            unit_banks = unit_cols // BANK
            for a in range(O_TILES):
                tiles = 1 if u < 3 else 2
                if a % tiles == 0:
                    stage = stages.tile([P, 2 * MAX_FRAMES * T], F32, name="stage")
                for i in range(unit_banks):
                    slot = a * unit_banks + i
                    if u == 0:
                        weave_first(slot)
                    else:
                        weave(u, slot)
                    cols = slice(i * BANK, (i + 1) * BANK)
                    place = a % tiles * unit_cols + i * BANK
                    stage_cols = slice(place, place + BANK)
                    bank = banks.tile([P, BANK], F32, name="bank")
                    nc.tensor.matmul_mx(
                        out=bank[:],
                        lhsT=wr_words[:, a * P : (a + 1) * P].bitcast(FP8X4),
                        lhsT_scale=wr_scales[:, a * P : (a + 1) * P],
                        rhs=d_words_of[u][:, cols].bitcast(FP8X4),
                        rhs_scale=d_scales_of[u][:, cols],
                        start=True,
                        stop=True,
                    )
                    if slot in (SCALAR_SLOTS[frames] if u > 0 else SCALAR_SLOTS_FIRST):
                        nc.scalar.activation(
                            out=stage[:, stage_cols],
                            in_=bank[:],
                            func=ACT.Identity,
                            bias=br_f32[:, a : a + 1],
                            scale=1.0,
                        )
                    else:
                        nc.vector.tensor_scalar(
                            out=stage[:, stage_cols],
                            in0=bank[:],
                            scalar1=br_f32[:, a : a + 1],
                            scalar2=None,
                            op0=ALU.add,
                        )
                if a % tiles == tiles - 1:
                    nc.sync.dma_start(
                        out=out_v[n, :, a + 1 - tiles : a + 1, first * T : first * T + unit_cols],
                        in_=stage[:, 0 : tiles * unit_cols].rearrange("p (a c) -> p a c", a=tiles),
                    )
